import numpy as np
import ml_dtypes


def mxq(x, axis, fmt="e4m3"):
    dtype, down = {"e4m3": (ml_dtypes.float8_e4m3fn, 7), "e5m2": (ml_dtypes.float8_e5m2, 14)}[fmt]
    v = np.moveaxis(np.asarray(x, np.float32).astype(ml_dtypes.bfloat16).astype(np.float64), axis, -1)
    blocks = v.reshape(v.shape[:-1] + (-1, 32))
    amax = np.abs(blocks).max(-1, keepdims=True)
    byte = np.maximum(np.where(amax > 0, np.frexp(amax)[1] - 1 + 127, 0) - down, 1)
    scale = np.exp2(byte - 127.0)
    codes = (blocks / scale).astype(np.float32).astype(dtype).astype(np.float64)
    return np.moveaxis((codes * scale).reshape(v.shape), -1, axis)


WIDE = False


def mx_kscale(k):
    if not WIDE:
        return np.ones(k)
    levels = np.array([10, -10, 5, -5, 0])
    a = np.random.permutation(np.resize(levels, k // 512 * 4)).reshape(k // 512, 4)
    idx = np.arange(k)
    return np.exp2(a[idx // 512, idx % 128 // 32])


BF16 = ml_dtypes.bfloat16


def bf(x):
    return np.asarray(x, np.float32).astype(BF16)


def f64(x):
    return np.asarray(x).astype(np.float64)


B, T, HP, WP, NH, D, DFF = 16, 8, 3, 4, 16, 1024, 4096
HW = HP * WP
D3 = D + D + D
EPS = 1e-6


def layer_norm(x, g, b):
    m = x.mean(-1, keepdims=True)
    v = np.square(x - m).mean(-1, keepdims=True)
    return (x - m) / np.sqrt(v + EPS) * g + b


def setup_inputs():
    s = mx_kscale(D)
    return {"x_res": bf(np.random.standard_normal((B, 1 + HW * T, D)) * 1.1),
            "ln1_g": bf((1.0 + 0.1 * np.random.standard_normal(D)) * s),
            "ln1_b": bf(0.1 * np.random.standard_normal(D) * s),
            "s_qkv_w": bf(np.random.standard_normal((D, D3)) / np.sqrt(D) / s[:, None]),
            "s_qkv_b": bf(0.1 * np.random.standard_normal(D3))}


def reference(x_res, ln1_g, ln1_b, s_qkv_w, s_qkv_b):
    x = f64(x_res)
    cls_rep = np.broadcast_to(x[:, 0:1, :], (B, T, D)).reshape(B * T, 1, D)
    xs = x[:, 1:, :].reshape(B, HW, T, D).swapaxes(1, 2).reshape(B * T, HW, D)
    xs = np.concatenate([cls_rep, xs], axis=1)
    y = layer_norm(xs, f64(ln1_g), f64(ln1_b))
    return (mxq(y, 2, "e4m3") @ mxq(f64(s_qkv_w), 0, "e4m3")) + f64(s_qkv_b)

@@ -1,0 +1,239 @@
+from contextlib import ExitStack
+
+import concourse.mybir as mybir
+from concourse.masks import make_identity
+
+F32 = mybir.dt.float32
+BF16 = mybir.dt.bfloat16
+U32 = mybir.dt.uint32
+U8 = mybir.dt.uint8
+FP8X4 = mybir.dt.float8_e4m3fn_x4
+ACT = mybir.ActivationFunctionType
+ALU = mybir.AluOpType
+
+P = 128
+PACK = 4
+SAMPLES, FRAMES, PATCHES = 16, 8, 12
+SEQ = 1 + PATCHES
+D = 1024
+D3 = 3072
+PASSES = D // (P * PACK)
+K_CHUNKS = D // P
+N_TILE = 512
+W_CHUNKS = D3 // N_TILE
+EPS = 1e-6
+FIRST_STEP = -2
+FLOPS = 2 * P * SEQ * D * D3
+
+
+def tile_timesformerlayer_pb_kernel(tc, x_res, ln1_g, ln1_b, s_qkv_w, s_qkv_b, out):
+    nc = tc.nc
+    with ExitStack() as ctx:
+        const = ctx.enter_context(tc.tile_pool(name="const", bufs=1))
+        keep = ctx.enter_context(tc.tile_pool(name="keep", bufs=1))
+        small = ctx.enter_context(tc.tile_pool(name="small", bufs=4))
+        work = ctx.enter_context(tc.tile_pool(name="work", bufs=3))
+        results = ctx.enter_context(tc.tile_pool(name="results", bufs=8))
+        turn_psum = ctx.enter_context(tc.psum_pool(name="turn_psum", bufs=2))
+        acc_psum = ctx.enter_context(tc.psum_pool(name="acc_psum", bufs=6))
+
+        w_view = s_qkv_w.rearrange("(j p) n -> p j n", p=P)
+        x_rows = [keep.tile([P, D], BF16, name="x%d" % s) for s in range(SEQ)]
+        w_raw = [keep.tile([P, K_CHUNKS, N_TILE], BF16, name="w_raw%d" % n) for n in range(W_CHUNKS)]
+        bias_rows = const.tile([P, D3], BF16)
+
+        def load_rows(s):
+            if s == 0:
+                source = x_res[:, 0:1, :].to_broadcast([SAMPLES, FRAMES, D])
+            else:
+                first = 1 + (s - 1) * FRAMES
+                source = x_res[:, first : first + FRAMES, :]
+            nc.sync.dma_start(out=x_rows[s][:], in_=source)
+
+        def load_weights(n):
+            cols = slice(n * N_TILE, (n + 1) * N_TILE)
+            nc.sync.dma_start(out=w_raw[n][:], in_=w_view[:, :, cols])
+            nc.sync.dma_start(out=bias_rows[:, cols], in_=s_qkv_b[cols].partition_broadcast(P))
+
+        def tiles_ahead(step):
+            return [s for s in (2 * step + 6, 2 * step + 7) if s < SEQ]
+
+        with tc.manual_schedule():
+            load_rows(0)
+            load_weights(0)
+            load_rows(1)
+            for step in range(FIRST_STEP, SEQ):
+                for s in tiles_ahead(step):
+                    load_rows(s)
+                if step + 3 < W_CHUNKS:
+                    load_weights(step + 3)
+
+        ident = const.tile([P, P], F32)
+        make_identity(nc, ident[:])
+        gs_rows_bf = const.tile([P, P], BF16)
+        nc.vector.memset(gs_rows_bf[:], 0.0)
+        nc.scalar.dma_start(out=gs_rows_bf[0:K_CHUNKS, :], in_=ln1_g.rearrange("(j p) -> j p", p=P))
+        nc.scalar.dma_start(
+            out=gs_rows_bf[K_CHUNKS : 2 * K_CHUNKS, :], in_=ln1_b.rearrange("(j p) -> j p", p=P)
+        )
+        gs_rows = const.tile([P, P], F32)
+        nc.vector.tensor_copy(out=gs_rows[:], in_=gs_rows_bf[:])
+        gs_turned = turn_psum.tile([P, PACK, P], F32, tag="turned")
+        nc.tensor.transpose(gs_turned[:, 0, :], gs_rows[:], ident[:])
+        gain_shift = const.tile([P, 2 * K_CHUNKS], F32)
+        nc.vector.tensor_copy(out=gain_shift[:], in_=gs_turned[:, 0, 0 : 2 * K_CHUNKS])
+
+        w_codes = keep.tile([P, W_CHUNKS, PASSES, N_TILE], U32, align_bytes=64)
+        w_scales = keep.tile([P, W_CHUNKS, PASSES, N_TILE], U8, align_bytes=64)
+        y_codes = [keep.tile([P, PASSES * P], U32, name="y_codes%d" % s, align_bytes=64) for s in range(SEQ)]
+        y_scales = [keep.tile([P, PASSES * P], U8, name="y_scales%d" % s, align_bytes=64) for s in range(SEQ)]
+        neg_mean = [keep.tile([P, 1], F32, name="neg_mean%d" % s) for s in range(SEQ)]
+        inv_var = [keep.tile([P, 1], F32, name="inv_var%d" % s) for s in range(SEQ)]
+        rstd = [keep.tile([P, 1], F32, name="rstd%d" % s) for s in range(SEQ)]
+        offset = [keep.tile([P, 1], F32, name="offset%d" % s) for s in range(SEQ)]
+        x_hat = {}
+        turned = {}
+        y_turned = {}
+        y_grouped = {}
+        w_grouped = {}
+
+        def moments(s):
+            stats = small.tile([P, 2, 6], F32)
+            half = D // 2
+            for h in range(2):
+                nc.vector.bn_stats(out=stats[:, h, :], in_=x_rows[s][:, h * half : (h + 1) * half])
+            mean_var = small.tile([P, 2], F32)
+            nc.vector.bn_aggr(out=mean_var[:], in_=stats[:].rearrange("p h c -> p (h c)"))
+            var_eps = small.tile([P, 1], F32)
+            nc.vector.tensor_scalar(out=var_eps[:], in0=mean_var[:, 1:2], scalar1=EPS, scalar2=None, op0=ALU.add)
+            nc.vector.tensor_scalar(out=neg_mean[s][:], in0=mean_var[:, 0:1], scalar1=-1.0, scalar2=None, op0=ALU.mult)
+            nc.vector.reciprocal(out=inv_var[s][:], in_=var_eps[:])
+
+        def row_scale(s):
+            nc.scalar.activation(out=rstd[s][:], in_=inv_var[s][:], func=ACT.Sqrt)
+
+        def row_offset(s):
+            nc.scalar.activation(out=offset[s][:], in_=neg_mean[s][:], func=ACT.Identity, scale=rstd[s][:])
+
+        def normalise(s):
+            x_hat[s] = work.tile([P, D], F32, name="x_hat")
+            nc.scalar.activation(
+                out=x_hat[s][:], in_=x_rows[s][:], func=ACT.Identity, bias=offset[s][:], scale=rstd[s][:]
+            )
+
+        def turn(s):
+            for c in range(PASSES):
+                turned[s, c] = turn_psum.tile([P, PACK, P], F32, name="turned", tag="turned")
+                for t in range(PACK):
+                    j = c * PACK + t
+                    nc.tensor.transpose(turned[s, c][:, t, :], x_hat[s][:, j * P : (j + 1) * P], ident[:])
+            y_turned[s] = work.tile([P, PASSES, PACK, P], BF16, name="y_turned")
+
+        def gain_and_shift(s, c):
+            for t in range(PACK):
+                j = c * PACK + t
+                nc.scalar.activation(
+                    out=y_turned[s][:, c, t, :],
+                    in_=turned[s, c][:, t, :],
+                    func=ACT.Identity,
+                    bias=gain_shift[:, K_CHUNKS + j : K_CHUNKS + j + 1],
+                    scale=gain_shift[:, j : j + 1],
+                )
+
+        def group_rows(s):
+            y_grouped[s] = work.tile([P, PASSES, P, PACK], BF16, name="y_grouped", align_bytes=64)
+            nc.gpsimd.tensor_scalar(
+                out=y_grouped[s][:],
+                in0=y_turned[s][:].rearrange("p c t r -> p c r t"),
+                scalar1=1.0,
+                scalar2=0.0,
+                op0=ALU.mult,
+                op1=ALU.add,
+            )
+
+        def pack_rows(s):
+            nc.vector.quantize_mx(
+                out=y_codes[s][:].bitcast(FP8X4),
+                scales=y_scales[s][:],
+                in_=y_grouped[s][:].rearrange("p c r t -> p (c r t)"),
+            )
+
+        def group_weights(n):
+            w_grouped[n, 0] = work.tile([P, N_TILE, PACK], BF16, name="w_grouped0", align_bytes=64)
+            nc.scalar.copy(
+                out=w_grouped[n, 0][:].rearrange("p (q i) t -> p q t i", i=4),
+                in_=w_raw[n][:, 0:PACK, :].rearrange("p t (q i) -> p q t i", i=4),
+            )
+            w_grouped[n, 1] = work.tile([P, N_TILE, PACK], BF16, name="w_grouped1", align_bytes=64)
+            nc.gpsimd.tensor_scalar(
+                out=w_grouped[n, 1][:],
+                in0=w_raw[n][:, PACK : 2 * PACK, :].rearrange("p t n -> p n t"),
+                scalar1=1.0,
+                scalar2=0.0,
+                op0=ALU.mult,
+                op1=ALU.add,
+            )
+
+        def pack_weights(n):
+            for c in range(PASSES):
+                nc.vector.quantize_mx(
+                    out=w_codes[:, n, c, :].bitcast(FP8X4),
+                    scales=w_scales[:, n, c, :],
+                    in_=w_grouped[n, c][:].rearrange("p n t -> p (n t)"),
+                )
+
+        def multiply(s, n):
+            acc = acc_psum.tile([P, N_TILE], F32)
+            for c in range(PASSES):
+                nc.tensor.matmul_mx(
+                    out=acc[:],
+                    lhsT=y_codes[s][:, c * P : (c + 1) * P].bitcast(FP8X4),
+                    lhsT_scale=y_scales[s][:, c * P : (c + 1) * P],
+                    rhs=w_codes[:, n, c, :].bitcast(FP8X4),
+                    rhs_scale=w_scales[:, n, c, :],
+                    start=(c == 0),
+                    stop=(c == PASSES - 1),
+                )
+            cols = slice(n * N_TILE, (n + 1) * N_TILE)
+            result = results.tile([P, N_TILE], F32)
+            nc.vector.tensor_tensor(out=result[:], in0=acc[:], in1=bias_rows[:, cols], op=ALU.add)
+            nc.sync.dma_start(out=out[:, s, cols], in_=result[:])
+
+        def new_pairs(step):
+            if step < 0:
+                return []
+            pairs = [(s, step) for s in range(step)] if step < W_CHUNKS else []
+            return pairs + [(step, n) for n in range(min(step + 1, W_CHUNKS))]
+
+        with tc.manual_schedule():
+            moments(0)
+            row_scale(0)
+            row_offset(0)
+            moments(1)
+            for step in range(FIRST_STEP, SEQ):
+                pairs = new_pairs(step)
+                middle = (len(pairs) + 1) // 2
+                if step + 2 < SEQ:
+                    normalise(step + 2)
+                if step + 2 < W_CHUNKS:
+                    group_weights(step + 2)
+                if step + 3 < SEQ:
+                    row_scale(step + 3)
+                for s, n in pairs[:middle]:
+                    multiply(s, n)
+                if step + 2 < SEQ:
+                    turn(step + 2)
+                    gain_and_shift(step + 2, 0)
+                if step + 3 < SEQ:
+                    row_offset(step + 3)
+                if step + 2 < SEQ:
+                    gain_and_shift(step + 2, 1)
+                    group_rows(step + 2)
+                if 0 <= step + 1 < W_CHUNKS:
+                    pack_weights(step + 1)
+                if 0 <= step + 1 < SEQ:
+                    pack_rows(step + 1)
+                for s in tiles_ahead(step):
+                    moments(s)
+                for s, n in pairs[middle:]:
+                    multiply(s, n)

@@ -22,7 +22,8 @@ K_CHUNKS = D // P
 N_TILE = 512
 W_CHUNKS = D3 // N_TILE
 EPS = 1e-6
-FIRST_STEP = -2
+FIRST_STEP = -4
+STORE_CHUNKS = 3
 FLOPS = 2 * P * SEQ * D * D3
 
 
@@ -33,7 +34,7 @@ def tile_timesformerlayer_pb_kernel(tc, x_res, ln1_g, ln1_b, s_qkv_w, s_qkv_b, o
         keep = ctx.enter_context(tc.tile_pool(name="keep", bufs=1))
         small = ctx.enter_context(tc.tile_pool(name="small", bufs=4))
         work = ctx.enter_context(tc.tile_pool(name="work", bufs=3))
-        results = ctx.enter_context(tc.tile_pool(name="results", bufs=8))
+        results = ctx.enter_context(tc.tile_pool(name="results", bufs=6))
         turn_psum = ctx.enter_context(tc.psum_pool(name="turn_psum", bufs=2))
         acc_psum = ctx.enter_context(tc.psum_pool(name="acc_psum", bufs=6))
 
@@ -55,21 +56,17 @@ def tile_timesformerlayer_pb_kernel(tc, x_res, ln1_g, ln1_b, s_qkv_w, s_qkv_b, o
             nc.sync.dma_start(out=w_raw[n][:], in_=w_view[:, :, cols])
             nc.sync.dma_start(out=bias_rows[:, cols], in_=s_qkv_b[cols].partition_broadcast(P))
 
-        def tiles_ahead(step):
-            return [s for s in (2 * step + 6, 2 * step + 7) if s < SEQ]
-
         with tc.manual_schedule():
-            load_rows(0)
-            load_weights(0)
-            load_rows(1)
             for step in range(FIRST_STEP, SEQ):
-                for s in tiles_ahead(step):
-                    load_rows(s)
-                if step + 3 < W_CHUNKS:
+                if step + 4 < SEQ:
+                    load_rows(step + 4)
+                if 0 <= step + 3 < W_CHUNKS:
                     load_weights(step + 3)
 
         ident = const.tile([P, P], F32)
         make_identity(nc, ident[:])
+        minus_half = const.tile([P, 1], F32)
+        nc.vector.memset(minus_half[:], -0.5)
         gs_rows_bf = const.tile([P, P], BF16)
         nc.vector.memset(gs_rows_bf[:], 0.0)
         nc.scalar.dma_start(out=gs_rows_bf[0:K_CHUNKS, :], in_=ln1_g.rearrange("(j p) -> j p", p=P))
@@ -87,8 +84,8 @@ def tile_timesformerlayer_pb_kernel(tc, x_res, ln1_g, ln1_b, s_qkv_w, s_qkv_b, o
         w_scales = keep.tile([P, W_CHUNKS, PASSES, N_TILE], U8, align_bytes=64)
         y_codes = [keep.tile([P, PASSES * P], U32, name="y_codes%d" % s, align_bytes=64) for s in range(SEQ)]
         y_scales = [keep.tile([P, PASSES * P], U8, name="y_scales%d" % s, align_bytes=64) for s in range(SEQ)]
-        neg_mean = [keep.tile([P, 1], F32, name="neg_mean%d" % s) for s in range(SEQ)]
-        inv_var = [keep.tile([P, 1], F32, name="inv_var%d" % s) for s in range(SEQ)]
+        stats = [keep.tile([P, 2, 6], F32, name="stats%d" % s) for s in range(SEQ)]
+        mean_var = [keep.tile([P, 2], F32, name="mean_var%d" % s) for s in range(SEQ)]
         rstd = [keep.tile([P, 1], F32, name="rstd%d" % s) for s in range(SEQ)]
         offset = [keep.tile([P, 1], F32, name="offset%d" % s) for s in range(SEQ)]
         x_hat = {}
@@ -97,23 +94,23 @@ def tile_timesformerlayer_pb_kernel(tc, x_res, ln1_g, ln1_b, s_qkv_w, s_qkv_b, o
         y_grouped = {}
         w_grouped = {}
 
-        def moments(s):
-            stats = small.tile([P, 2, 6], F32)
+        def row_sums(s):
             half = D // 2
             for h in range(2):
-                nc.vector.bn_stats(out=stats[:, h, :], in_=x_rows[s][:, h * half : (h + 1) * half])
-            mean_var = small.tile([P, 2], F32)
-            nc.vector.bn_aggr(out=mean_var[:], in_=stats[:].rearrange("p h c -> p (h c)"))
+                nc.vector.bn_stats(out=stats[s][:, h, :], in_=x_rows[s][:, h * half : (h + 1) * half])
+
+        def row_moments(s):
+            nc.vector.bn_aggr(out=mean_var[s][:], in_=stats[s][:].rearrange("p h c -> p (h c)"))
+
+        def row_factors(s):
             var_eps = small.tile([P, 1], F32)
-            nc.vector.tensor_scalar(out=var_eps[:], in0=mean_var[:, 1:2], scalar1=EPS, scalar2=None, op0=ALU.add)
-            nc.vector.tensor_scalar(out=neg_mean[s][:], in0=mean_var[:, 0:1], scalar1=-1.0, scalar2=None, op0=ALU.mult)
-            nc.vector.reciprocal(out=inv_var[s][:], in_=var_eps[:])
-
-        def row_scale(s):
-            nc.scalar.activation(out=rstd[s][:], in_=inv_var[s][:], func=ACT.Sqrt)
-
-        def row_offset(s):
-            nc.scalar.activation(out=offset[s][:], in_=neg_mean[s][:], func=ACT.Identity, scale=rstd[s][:])
+            nc.gpsimd.tensor_scalar(
+                out=var_eps[:], in0=mean_var[s][:, 1:2], scalar1=1.0, scalar2=EPS, op0=ALU.mult, op1=ALU.add
+            )
+            nc.gpsimd.tensor_tensor(out=rstd[s][:], in0=var_eps[:], in1=minus_half[:], op=ALU.pow)
+            nc.gpsimd.tensor_scalar(
+                out=offset[s][:], in0=mean_var[s][:, 0:1], scalar1=rstd[s][:], scalar2=-1.0, op0=ALU.mult, op1=ALU.mult
+            )
 
         def normalise(s):
             x_hat[s] = work.tile([P, D], F32, name="x_hat")
@@ -182,58 +179,63 @@ def tile_timesformerlayer_pb_kernel(tc, x_res, ln1_g, ln1_b, s_qkv_w, s_qkv_b, o
                     in_=w_grouped[n, c][:].rearrange("p n t -> p (n t)"),
                 )
 
-        def multiply(s, n):
-            acc = acc_psum.tile([P, N_TILE], F32)
-            for c in range(PASSES):
-                nc.tensor.matmul_mx(
-                    out=acc[:],
-                    lhsT=y_codes[s][:, c * P : (c + 1) * P].bitcast(FP8X4),
-                    lhsT_scale=y_scales[s][:, c * P : (c + 1) * P],
-                    rhs=w_codes[:, n, c, :].bitcast(FP8X4),
-                    rhs_scale=w_scales[:, n, c, :],
-                    start=(c == 0),
-                    stop=(c == PASSES - 1),
+        def multiply(s, first, count):
+            result = results.tile([P, STORE_CHUNKS * N_TILE], F32)
+            for i in range(count):
+                n = first + i
+                acc = acc_psum.tile([P, N_TILE], F32)
+                for c in range(PASSES):
+                    nc.tensor.matmul_mx(
+                        out=acc[:],
+                        lhsT=y_codes[s][:, c * P : (c + 1) * P].bitcast(FP8X4),
+                        lhsT_scale=y_scales[s][:, c * P : (c + 1) * P],
+                        rhs=w_codes[:, n, c, :].bitcast(FP8X4),
+                        rhs_scale=w_scales[:, n, c, :],
+                        start=(c == 0),
+                        stop=(c == PASSES - 1),
+                    )
+                nc.vector.tensor_tensor(
+                    out=result[:, i * N_TILE : (i + 1) * N_TILE],
+                    in0=acc[:],
+                    in1=bias_rows[:, n * N_TILE : (n + 1) * N_TILE],
+                    op=ALU.add,
                 )
-            cols = slice(n * N_TILE, (n + 1) * N_TILE)
-            result = results.tile([P, N_TILE], F32)
-            nc.vector.tensor_tensor(out=result[:], in0=acc[:], in1=bias_rows[:, cols], op=ALU.add)
-            nc.sync.dma_start(out=out[:, s, cols], in_=result[:])
+            nc.sync.dma_start(
+                out=out[:, s, first * N_TILE : (first + count) * N_TILE], in_=result[:, 0 : count * N_TILE]
+            )
 
-        def new_pairs(step):
+        def new_products(step):
             if step < 0:
                 return []
-            pairs = [(s, step) for s in range(step)] if step < W_CHUNKS else []
-            return pairs + [(step, n) for n in range(min(step + 1, W_CHUNKS))]
+            column = [(s, step, 1) for s in range(step)] if step < W_CHUNKS else []
+            chunks = min(step + 1, W_CHUNKS)
+            row = [(step, first, min(STORE_CHUNKS, chunks - first)) for first in range(0, chunks, STORE_CHUNKS)]
+            return column + row
 
         with tc.manual_schedule():
-            moments(0)
-            row_scale(0)
-            row_offset(0)
-            moments(1)
             for step in range(FIRST_STEP, SEQ):
-                pairs = new_pairs(step)
-                middle = (len(pairs) + 1) // 2
-                if step + 2 < SEQ:
+                products = new_products(step)
+                middle = (len(products) + 1) // 2
+                if 0 <= step + 2 < SEQ:
                     normalise(step + 2)
-                if step + 2 < W_CHUNKS:
+                if 0 <= step + 2 < W_CHUNKS:
                     group_weights(step + 2)
-                if step + 3 < SEQ:
-                    row_scale(step + 3)
-                for s, n in pairs[:middle]:
-                    multiply(s, n)
-                if step + 2 < SEQ:
+                if 0 <= step + 3 < SEQ:
+                    row_factors(step + 3)
+                for s, first, count in products[:middle]:
+                    multiply(s, first, count)
+                if 0 <= step + 2 < SEQ:
                     turn(step + 2)
                     gain_and_shift(step + 2, 0)
-                if step + 3 < SEQ:
-                    row_offset(step + 3)
-                if step + 2 < SEQ:
                     gain_and_shift(step + 2, 1)
                     group_rows(step + 2)
                 if 0 <= step + 1 < W_CHUNKS:
                     pack_weights(step + 1)
                 if 0 <= step + 1 < SEQ:
                     pack_rows(step + 1)
-                for s in tiles_ahead(step):
-                    moments(s)
-                for s, n in pairs[middle:]:
-                    multiply(s, n)
+                if step + 4 < SEQ:
+                    row_sums(step + 4)
+                for s, first, count in products[middle:]:
+                    multiply(s, first, count)
+                if step + 4 < SEQ:
+                    row_moments(step + 4)

@@ -41,7 +41,6 @@ def tile_timesformerlayer_pb_kernel(tc, x_res, ln1_g, ln1_b, s_qkv_w, s_qkv_b, o
         w_view = s_qkv_w.rearrange("(j p) n -> p j n", p=P)
         x_rows = [keep.tile([P, D], BF16, name="x%d" % s) for s in range(SEQ)]
         w_raw = [keep.tile([P, K_CHUNKS, N_TILE], BF16, name="w_raw%d" % n) for n in range(W_CHUNKS)]
-        bias_rows = const.tile([P, D3], BF16)
 
         def load_rows(s):
             if s == 0:
@@ -54,7 +53,6 @@ def tile_timesformerlayer_pb_kernel(tc, x_res, ln1_g, ln1_b, s_qkv_w, s_qkv_b, o
         def load_weights(n):
             cols = slice(n * N_TILE, (n + 1) * N_TILE)
             nc.sync.dma_start(out=w_raw[n][:], in_=w_view[:, :, cols])
-            nc.sync.dma_start(out=bias_rows[:, cols], in_=s_qkv_b[cols].partition_broadcast(P))
 
         with tc.manual_schedule():
             for step in range(FIRST_STEP, SEQ):
@@ -79,6 +77,18 @@ def tile_timesformerlayer_pb_kernel(tc, x_res, ln1_g, ln1_b, s_qkv_w, s_qkv_b, o
         nc.tensor.transpose(gs_turned[:, 0, :], gs_rows[:], ident[:])
         gain_shift = const.tile([P, 2 * K_CHUNKS], F32)
         nc.vector.tensor_copy(out=gain_shift[:], in_=gs_turned[:, 0, 0 : 2 * K_CHUNKS])
+
+        bias_row = const.tile([P, D3], BF16)
+        nc.vector.memset(bias_row[:], 0.0)
+        nc.scalar.dma_start(out=bias_row[0:1, :], in_=s_qkv_b.unsqueeze(0))
+        ones = const.tile([P, P], BF16)
+        nc.vector.memset(ones[:], 1.0)
+        bias_rows = const.tile([P, D3], BF16)
+        for n in range(W_CHUNKS):
+            cols = slice(n * N_TILE, (n + 1) * N_TILE)
+            spread = acc_psum.tile([P, N_TILE], F32, tag="acc")
+            nc.tensor.matmul(out=spread[:], lhsT=ones[:], rhs=bias_row[:, cols], start=True, stop=True)
+            nc.scalar.copy(out=bias_rows[:, cols], in_=spread[:])
 
         w_codes = keep.tile([P, W_CHUNKS, PASSES, N_TILE], U32, align_bytes=64)
         w_scales = keep.tile([P, W_CHUNKS, PASSES, N_TILE], U8, align_bytes=64)
@@ -183,7 +193,7 @@ def tile_timesformerlayer_pb_kernel(tc, x_res, ln1_g, ln1_b, s_qkv_w, s_qkv_b, o
             result = results.tile([P, STORE_CHUNKS * N_TILE], F32)
             for i in range(count):
                 n = first + i
-                acc = acc_psum.tile([P, N_TILE], F32)
+                acc = acc_psum.tile([P, N_TILE], F32, tag="acc")
                 for c in range(PASSES):
                     nc.tensor.matmul_mx(
                         out=acc[:],

@@ -32,7 +32,6 @@ def tile_timesformerlayer_pb_kernel(tc, x_res, ln1_g, ln1_b, s_qkv_w, s_qkv_b, o
     with ExitStack() as ctx:
         const = ctx.enter_context(tc.tile_pool(name="const", bufs=1))
         keep = ctx.enter_context(tc.tile_pool(name="keep", bufs=1))
-        small = ctx.enter_context(tc.tile_pool(name="small", bufs=4))
         work = ctx.enter_context(tc.tile_pool(name="work", bufs=3))
         results = ctx.enter_context(tc.tile_pool(name="results", bufs=6))
         turn_psum = ctx.enter_context(tc.psum_pool(name="turn_psum", bufs=2))
@@ -41,6 +40,7 @@ def tile_timesformerlayer_pb_kernel(tc, x_res, ln1_g, ln1_b, s_qkv_w, s_qkv_b, o
         w_view = s_qkv_w.rearrange("(j p) n -> p j n", p=P)
         x_rows = [keep.tile([P, D], BF16, name="x%d" % s) for s in range(SEQ)]
         w_raw = [keep.tile([P, K_CHUNKS, N_TILE], BF16, name="w_raw%d" % n) for n in range(W_CHUNKS)]
+        bias_rows = const.tile([P, D3], BF16)
 
         def load_rows(s):
             if s == 0:
@@ -53,6 +53,7 @@ def tile_timesformerlayer_pb_kernel(tc, x_res, ln1_g, ln1_b, s_qkv_w, s_qkv_b, o
         def load_weights(n):
             cols = slice(n * N_TILE, (n + 1) * N_TILE)
             nc.sync.dma_start(out=w_raw[n][:], in_=w_view[:, :, cols])
+            nc.sync.dma_start(out=bias_rows[:, cols], in_=s_qkv_b[cols].partition_broadcast(P))
 
         with tc.manual_schedule():
             for step in range(FIRST_STEP, SEQ):
@@ -63,8 +64,8 @@ def tile_timesformerlayer_pb_kernel(tc, x_res, ln1_g, ln1_b, s_qkv_w, s_qkv_b, o
 
         ident = const.tile([P, P], F32)
         make_identity(nc, ident[:])
-        minus_half = const.tile([P, 1], F32)
-        nc.vector.memset(minus_half[:], -0.5)
+        eps = const.tile([P, 1], F32)
+        nc.vector.memset(eps[:], EPS)
         gs_rows_bf = const.tile([P, P], BF16)
         nc.vector.memset(gs_rows_bf[:], 0.0)
         nc.scalar.dma_start(out=gs_rows_bf[0:K_CHUNKS, :], in_=ln1_g.rearrange("(j p) -> j p", p=P))
@@ -77,18 +78,6 @@ def tile_timesformerlayer_pb_kernel(tc, x_res, ln1_g, ln1_b, s_qkv_w, s_qkv_b, o
         nc.tensor.transpose(gs_turned[:, 0, :], gs_rows[:], ident[:])
         gain_shift = const.tile([P, 2 * K_CHUNKS], F32)
         nc.vector.tensor_copy(out=gain_shift[:], in_=gs_turned[:, 0, 0 : 2 * K_CHUNKS])
-
-        bias_row = const.tile([P, D3], BF16)
-        nc.vector.memset(bias_row[:], 0.0)
-        nc.scalar.dma_start(out=bias_row[0:1, :], in_=s_qkv_b.unsqueeze(0))
-        ones = const.tile([P, P], BF16)
-        nc.vector.memset(ones[:], 1.0)
-        bias_rows = const.tile([P, D3], BF16)
-        for n in range(W_CHUNKS):
-            cols = slice(n * N_TILE, (n + 1) * N_TILE)
-            spread = acc_psum.tile([P, N_TILE], F32, tag="acc")
-            nc.tensor.matmul(out=spread[:], lhsT=ones[:], rhs=bias_row[:, cols], start=True, stop=True)
-            nc.scalar.copy(out=bias_rows[:, cols], in_=spread[:])
 
         w_codes = keep.tile([P, W_CHUNKS, PASSES, N_TILE], U32, align_bytes=64)
         w_scales = keep.tile([P, W_CHUNKS, PASSES, N_TILE], U8, align_bytes=64)
@@ -112,12 +101,12 @@ def tile_timesformerlayer_pb_kernel(tc, x_res, ln1_g, ln1_b, s_qkv_w, s_qkv_b, o
         def row_moments(s):
             nc.vector.bn_aggr(out=mean_var[s][:], in_=stats[s][:].rearrange("p h c -> p (h c)"))
 
-        def row_factors(s):
-            var_eps = small.tile([P, 1], F32)
-            nc.gpsimd.tensor_scalar(
-                out=var_eps[:], in0=mean_var[s][:, 1:2], scalar1=1.0, scalar2=EPS, op0=ALU.mult, op1=ALU.add
+        def row_scale(s):
+            nc.scalar.activation(
+                out=rstd[s][:], in_=mean_var[s][:, 1:2], func=ACT.Abs_reciprocal_sqrt, bias=eps[:], scale=1.0
             )
-            nc.gpsimd.tensor_tensor(out=rstd[s][:], in0=var_eps[:], in1=minus_half[:], op=ALU.pow)
+
+        def row_offset(s):
             nc.gpsimd.tensor_scalar(
                 out=offset[s][:], in0=mean_var[s][:, 0:1], scalar1=rstd[s][:], scalar2=-1.0, op0=ALU.mult, op1=ALU.mult
             )
@@ -193,7 +182,7 @@ def tile_timesformerlayer_pb_kernel(tc, x_res, ln1_g, ln1_b, s_qkv_w, s_qkv_b, o
             result = results.tile([P, STORE_CHUNKS * N_TILE], F32)
             for i in range(count):
                 n = first + i
-                acc = acc_psum.tile([P, N_TILE], F32, tag="acc")
+                acc = acc_psum.tile([P, N_TILE], F32)
                 for c in range(PASSES):
                     nc.tensor.matmul_mx(
                         out=acc[:],
@@ -204,12 +193,13 @@ def tile_timesformerlayer_pb_kernel(tc, x_res, ln1_g, ln1_b, s_qkv_w, s_qkv_b, o
                         start=(c == 0),
                         stop=(c == PASSES - 1),
                     )
-                nc.vector.tensor_tensor(
-                    out=result[:, i * N_TILE : (i + 1) * N_TILE],
-                    in0=acc[:],
-                    in1=bias_rows[:, n * N_TILE : (n + 1) * N_TILE],
-                    op=ALU.add,
-                )
+                part = result[:, i * N_TILE : (i + 1) * N_TILE]
+                bias_part = bias_rows[:, n * N_TILE : (n + 1) * N_TILE]
+                if i < STORE_CHUNKS - 1:
+                    nc.vector.tensor_tensor(out=part, in0=acc[:], in1=bias_part, op=ALU.add)
+                else:
+                    nc.scalar.copy(out=part, in_=acc[:])
+                    nc.gpsimd.tensor_tensor(out=part, in0=part, in1=bias_part, op=ALU.add)
             nc.sync.dma_start(
                 out=out[:, s, first * N_TILE : (first + count) * N_TILE], in_=result[:, 0 : count * N_TILE]
             )
@@ -231,7 +221,8 @@ def tile_timesformerlayer_pb_kernel(tc, x_res, ln1_g, ln1_b, s_qkv_w, s_qkv_b, o
                 if 0 <= step + 2 < W_CHUNKS:
                     group_weights(step + 2)
                 if 0 <= step + 3 < SEQ:
-                    row_factors(step + 3)
+                    row_scale(step + 3)
+                    row_offset(step + 3)
                 for s, first, count in products[:middle]:
                     multiply(s, first, count)
                 if 0 <= step + 2 < SEQ:

@@ -22,9 +22,10 @@ K_CHUNKS = D // P
 N_TILE = 512
 W_CHUNKS = D3 // N_TILE
 EPS = 1e-6
-FIRST_STEP = -4
+FIRST_STEP = -5
 STORE_CHUNKS = 3
 FLOPS = 2 * P * SEQ * D * D3
+SHARE = 4
 
 
 def tile_timesformerlayer_pb_kernel(tc, x_res, ln1_g, ln1_b, s_qkv_w, s_qkv_b, out):
@@ -41,6 +42,8 @@ def tile_timesformerlayer_pb_kernel(tc, x_res, ln1_g, ln1_b, s_qkv_w, s_qkv_b, o
         x_rows = [keep.tile([P, D], BF16, name="x%d" % s) for s in range(SEQ)]
         w_raw = [keep.tile([P, K_CHUNKS, N_TILE], BF16, name="w_raw%d" % n) for n in range(W_CHUNKS)]
         bias_rows = const.tile([P, D3], BF16)
+        gs_rows_bf = const.tile([P, P], BF16)
+        nc.vector.memset(gs_rows_bf[:], 0.0)
 
         def load_rows(s):
             if s == 0:
@@ -50,34 +53,55 @@ def tile_timesformerlayer_pb_kernel(tc, x_res, ln1_g, ln1_b, s_qkv_w, s_qkv_b, o
                 source = x_res[:, first : first + FRAMES, :]
             nc.sync.dma_start(out=x_rows[s][:], in_=source)
 
+        def load_gain_shift():
+            nc.sync.dma_start(out=gs_rows_bf[0:K_CHUNKS, :], in_=ln1_g.rearrange("(j p) -> j p", p=P))
+            nc.sync.dma_start(out=gs_rows_bf[K_CHUNKS : 2 * K_CHUNKS, :], in_=ln1_b.rearrange("(j p) -> j p", p=P))
+
         def load_weights(n):
             cols = slice(n * N_TILE, (n + 1) * N_TILE)
             nc.sync.dma_start(out=w_raw[n][:], in_=w_view[:, :, cols])
+
+        def load_bias(n):
+            cols = slice(n * N_TILE, (n + 1) * N_TILE)
             nc.sync.dma_start(out=bias_rows[:, cols], in_=s_qkv_b[cols].partition_broadcast(P))
 
         with tc.manual_schedule():
-            for step in range(FIRST_STEP, SEQ):
-                if step + 4 < SEQ:
-                    load_rows(step + 4)
-                if 0 <= step + 3 < W_CHUNKS:
-                    load_weights(step + 3)
+            load_rows(0)
+            load_gain_shift()
+            load_rows(1)
+            load_weights(0)
+            load_rows(2)
+            load_bias(0)
+            load_weights(1)
+            load_rows(3)
+            load_bias(1)
+            load_weights(2)
+            load_rows(4)
+            load_bias(2)
+            load_weights(3)
+            load_rows(5)
+            load_bias(3)
+            load_weights(4)
+            load_rows(6)
+            load_bias(4)
+            load_weights(5)
+            load_rows(7)
+            load_bias(5)
+            for s in range(8, SEQ):
+                load_rows(s)
 
         ident = const.tile([P, P], F32)
         make_identity(nc, ident[:])
         eps = const.tile([P, 1], F32)
         nc.vector.memset(eps[:], EPS)
-        gs_rows_bf = const.tile([P, P], BF16)
-        nc.vector.memset(gs_rows_bf[:], 0.0)
-        nc.scalar.dma_start(out=gs_rows_bf[0:K_CHUNKS, :], in_=ln1_g.rearrange("(j p) -> j p", p=P))
-        nc.scalar.dma_start(
-            out=gs_rows_bf[K_CHUNKS : 2 * K_CHUNKS, :], in_=ln1_b.rearrange("(j p) -> j p", p=P)
-        )
         gs_rows = const.tile([P, P], F32)
-        nc.vector.tensor_copy(out=gs_rows[:], in_=gs_rows_bf[:])
-        gs_turned = turn_psum.tile([P, PACK, P], F32, tag="turned")
-        nc.tensor.transpose(gs_turned[:, 0, :], gs_rows[:], ident[:])
         gain_shift = const.tile([P, 2 * K_CHUNKS], F32)
-        nc.vector.tensor_copy(out=gain_shift[:], in_=gs_turned[:, 0, 0 : 2 * K_CHUNKS])
+
+        def turn_gain_shift():
+            nc.vector.tensor_copy(out=gs_rows[:], in_=gs_rows_bf[:])
+            gs_turned = turn_psum.tile([P, PACK, P], F32, name="gs_turned", tag="turned")
+            nc.tensor.transpose(gs_turned[:, 0, :], gs_rows[:], ident[:])
+            nc.vector.tensor_copy(out=gain_shift[:], in_=gs_turned[:, 0, 0 : 2 * K_CHUNKS])
 
         w_codes = keep.tile([P, W_CHUNKS, PASSES, N_TILE], U32, align_bytes=64)
         w_scales = keep.tile([P, W_CHUNKS, PASSES, N_TILE], U8, align_bytes=64)
@@ -93,10 +117,9 @@ def tile_timesformerlayer_pb_kernel(tc, x_res, ln1_g, ln1_b, s_qkv_w, s_qkv_b, o
         y_grouped = {}
         w_grouped = {}
 
-        def row_sums(s):
+        def row_sums(s, h):
             half = D // 2
-            for h in range(2):
-                nc.vector.bn_stats(out=stats[s][:, h, :], in_=x_rows[s][:, h * half : (h + 1) * half])
+            nc.vector.bn_stats(out=stats[s][:, h, :], in_=x_rows[s][:, h * half : (h + 1) * half])
 
         def row_moments(s):
             nc.vector.bn_aggr(out=mean_var[s][:], in_=stats[s][:].rearrange("p h c -> p (h c)"))
@@ -106,15 +129,10 @@ def tile_timesformerlayer_pb_kernel(tc, x_res, ln1_g, ln1_b, s_qkv_w, s_qkv_b, o
                 out=rstd[s][:], in_=mean_var[s][:, 1:2], func=ACT.Abs_reciprocal_sqrt, bias=eps[:], scale=1.0
             )
 
-        def row_offset(s):
-            nc.gpsimd.tensor_scalar(
-                out=offset[s][:], in0=mean_var[s][:, 0:1], scalar1=rstd[s][:], scalar2=-1.0, op0=ALU.mult, op1=ALU.mult
-            )
-
         def normalise(s):
             x_hat[s] = work.tile([P, D], F32, name="x_hat")
-            nc.scalar.activation(
-                out=x_hat[s][:], in_=x_rows[s][:], func=ACT.Identity, bias=offset[s][:], scale=rstd[s][:]
+            nc.gpsimd.tensor_scalar(
+                out=x_hat[s][:], in0=x_rows[s][:], scalar1=mean_var[s][:, 0:1], scalar2=rstd[s][:], op0=ALU.subtract, op1=ALU.mult
             )
 
         def turn(s):
@@ -138,14 +156,11 @@ def tile_timesformerlayer_pb_kernel(tc, x_res, ln1_g, ln1_b, s_qkv_w, s_qkv_b, o
 
         def group_rows(s):
             y_grouped[s] = work.tile([P, PASSES, P, PACK], BF16, name="y_grouped", align_bytes=64)
-            nc.gpsimd.tensor_scalar(
-                out=y_grouped[s][:],
-                in0=y_turned[s][:].rearrange("p c t r -> p c r t"),
-                scalar1=1.0,
-                scalar2=0.0,
-                op0=ALU.mult,
-                op1=ALU.add,
-            )
+            for c in range(PASSES):
+                nc.scalar.copy(
+                    out=y_grouped[s][:, c, :, :].rearrange("p (q i) t -> p q t i", i=4),
+                    in_=y_turned[s][:, c, :, :].rearrange("p t (q i) -> p q t i", i=4),
+                )
 
         def pack_rows(s):
             nc.vector.quantize_mx(
@@ -154,55 +169,65 @@ def tile_timesformerlayer_pb_kernel(tc, x_res, ln1_g, ln1_b, s_qkv_w, s_qkv_b, o
                 in_=y_grouped[s][:].rearrange("p c r t -> p (c r t)"),
             )
 
-        def group_weights(n):
-            w_grouped[n, 0] = work.tile([P, N_TILE, PACK], BF16, name="w_grouped0", align_bytes=64)
-            nc.scalar.copy(
-                out=w_grouped[n, 0][:].rearrange("p (q i) t -> p q t i", i=4),
-                in_=w_raw[n][:, 0:PACK, :].rearrange("p t (q i) -> p q t i", i=4),
-            )
-            w_grouped[n, 1] = work.tile([P, N_TILE, PACK], BF16, name="w_grouped1", align_bytes=64)
-            nc.gpsimd.tensor_scalar(
-                out=w_grouped[n, 1][:],
-                in0=w_raw[n][:, PACK : 2 * PACK, :].rearrange("p t n -> p n t"),
-                scalar1=1.0,
-                scalar2=0.0,
-                op0=ALU.mult,
-                op1=ALU.add,
-            )
-
-        def pack_weights(n):
-            for c in range(PASSES):
-                nc.vector.quantize_mx(
-                    out=w_codes[:, n, c, :].bitcast(FP8X4),
-                    scales=w_scales[:, n, c, :],
-                    in_=w_grouped[n, c][:].rearrange("p n t -> p (n t)"),
+        def group_weights(n, c):
+            w_grouped[n, c] = work.tile([P, N_TILE, PACK], BF16, name="w_grouped%d" % c, align_bytes=64)
+            if c == 1:
+                nc.gpsimd.tensor_scalar(
+                    out=w_grouped[n, c][:],
+                    in0=w_raw[n][:, c * PACK : (c + 1) * PACK, :].rearrange("p t n -> p n t"),
+                    scalar1=1.0,
+                    scalar2=0.0,
+                    op0=ALU.mult,
+                    op1=ALU.add,
+                )
+            elif n < 3:
+                nc.vector.tensor_copy(
+                    out=w_grouped[n, c][:].rearrange("p (q i) t -> p q t i", i=4),
+                    in_=w_raw[n][:, c * PACK : (c + 1) * PACK, :].rearrange("p t (q i) -> p q t i", i=4),
+                )
+            else:
+                nc.scalar.copy(
+                    out=w_grouped[n, c][:].rearrange("p (q i) t -> p q t i", i=4),
+                    in_=w_raw[n][:, c * PACK : (c + 1) * PACK, :].rearrange("p t (q i) -> p q t i", i=4),
                 )
 
-        def multiply(s, first, count):
-            result = results.tile([P, STORE_CHUNKS * N_TILE], F32)
-            for i in range(count):
-                n = first + i
-                acc = acc_psum.tile([P, N_TILE], F32)
-                for c in range(PASSES):
-                    nc.tensor.matmul_mx(
-                        out=acc[:],
-                        lhsT=y_codes[s][:, c * P : (c + 1) * P].bitcast(FP8X4),
-                        lhsT_scale=y_scales[s][:, c * P : (c + 1) * P],
-                        rhs=w_codes[:, n, c, :].bitcast(FP8X4),
-                        rhs_scale=w_scales[:, n, c, :],
-                        start=(c == 0),
-                        stop=(c == PASSES - 1),
-                    )
-                part = result[:, i * N_TILE : (i + 1) * N_TILE]
-                bias_part = bias_rows[:, n * N_TILE : (n + 1) * N_TILE]
-                if i < STORE_CHUNKS - 1:
-                    nc.vector.tensor_tensor(out=part, in0=acc[:], in1=bias_part, op=ALU.add)
-                else:
-                    nc.scalar.copy(out=part, in_=acc[:])
-                    nc.gpsimd.tensor_tensor(out=part, in0=part, in1=bias_part, op=ALU.add)
-            nc.sync.dma_start(
-                out=out[:, s, first * N_TILE : (first + count) * N_TILE], in_=result[:, 0 : count * N_TILE]
+        def pack_weights(n, c):
+            nc.vector.quantize_mx(
+                out=w_codes[:, n, c, :].bitcast(FP8X4),
+                scales=w_scales[:, n, c, :],
+                in_=w_grouped[n, c][:].rearrange("p n t -> p (n t)"),
             )
+
+        state = {"banks": 0, "result": None}
+
+        def multiply(s, n, place, count):
+            if place == 0:
+                state["result"] = (results.tile([P, count * N_TILE], F32, name="result%d" % count, bufs=[8,3,5][count - 1]))
+            result = state["result"]
+            acc = acc_psum.tile([P, N_TILE], F32, name="acc")
+            for c in range(PASSES):
+                nc.tensor.matmul_mx(
+                    out=acc[:],
+                    lhsT=y_codes[s][:, c * P : (c + 1) * P].bitcast(FP8X4),
+                    lhsT_scale=y_scales[s][:, c * P : (c + 1) * P],
+                    rhs=w_codes[:, n, c, :].bitcast(FP8X4),
+                    rhs_scale=w_scales[:, n, c, :],
+                    start=(c == 0),
+                    stop=(c == PASSES - 1),
+                )
+            part = result[:, place * N_TILE : (place + 1) * N_TILE]
+            bias_part = bias_rows[:, n * N_TILE : (n + 1) * N_TILE]
+            if state["banks"] % SHARE != SHARE - 1:
+                nc.vector.tensor_tensor(out=part, in0=acc[:], in1=bias_part, op=ALU.add)
+            else:
+                nc.scalar.copy(out=part, in_=acc[:])
+                nc.gpsimd.tensor_tensor(out=part, in0=part, in1=bias_part, op=ALU.add)
+            state["banks"] += 1
+            if place == count - 1:
+                first = n - place
+                nc.sync.dma_start(
+                    out=out[:, s, first * N_TILE : (first + count) * N_TILE], in_=result[:, 0 : count * N_TILE]
+                )
 
         def new_products(step):
             if step < 0:
@@ -214,29 +239,35 @@ def tile_timesformerlayer_pb_kernel(tc, x_res, ln1_g, ln1_b, s_qkv_w, s_qkv_b, o
 
         with tc.manual_schedule():
             for step in range(FIRST_STEP, SEQ):
-                products = new_products(step)
-                middle = (len(products) + 1) // 2
-                if 0 <= step + 2 < SEQ:
-                    normalise(step + 2)
-                if 0 <= step + 2 < W_CHUNKS:
-                    group_weights(step + 2)
-                if 0 <= step + 3 < SEQ:
-                    row_scale(step + 3)
-                    row_offset(step + 3)
-                for s, first, count in products[:middle]:
-                    multiply(s, first, count)
-                if 0 <= step + 2 < SEQ:
-                    turn(step + 2)
-                    gain_and_shift(step + 2, 0)
-                    gain_and_shift(step + 2, 1)
-                    group_rows(step + 2)
-                if 0 <= step + 1 < W_CHUNKS:
-                    pack_weights(step + 1)
-                if 0 <= step + 1 < SEQ:
-                    pack_rows(step + 1)
-                if step + 4 < SEQ:
-                    row_sums(step + 4)
-                for s, first, count in products[middle:]:
-                    multiply(s, first, count)
-                if step + 4 < SEQ:
-                    row_moments(step + 4)
+                banks = [(s, first + i, i, count) for s, first, count in new_products(step) for i in range(count)]
+                tasks = []
+
+                def add(ahead, limit, f, *args):
+                    if 0 <= step + ahead < limit:
+                        tasks.append(lambda: f(step + ahead, *args))
+
+                add(3, SEQ, row_scale)
+                add(3, SEQ, normalise)
+                add(1, SEQ, pack_rows)
+                add(2, W_CHUNKS, group_weights, 0)
+                add(2, W_CHUNKS, group_weights, 1)
+                add(1, W_CHUNKS, pack_weights, 0)
+                add(2, SEQ, turn)
+                add(2, SEQ, gain_and_shift, 0)
+                add(4, SEQ, row_sums, 0)
+                add(2, SEQ, gain_and_shift, 1)
+                add(2, SEQ, group_rows)
+                add(1, W_CHUNKS, pack_weights, 1)
+                add(4, SEQ, row_sums, 1)
+                add(4, SEQ, row_moments)
+                if step == FIRST_STEP + 1:
+                    tasks.append(turn_gain_shift)
+                done = 0
+                for b, bank in enumerate(banks):
+                    multiply(*bank)
+                    upto = ((b + 1) * len(tasks)) // len(banks)
+                    for task in tasks[done:upto]:
+                        task()
+                    done = upto
+                for task in tasks[done:]:
+                    task()

@@ -132,7 +132,10 @@ def tile_timesformerlayer_pb_kernel(tc, x_res, ln1_g, ln1_b, s_qkv_w, s_qkv_b, o
         def normalise(s):
             x_hat[s] = work.tile([P, D], F32, name="x_hat")
             nc.gpsimd.tensor_scalar(
-                out=x_hat[s][:], in0=x_rows[s][:], scalar1=mean_var[s][:, 0:1], scalar2=rstd[s][:], op0=ALU.subtract, op1=ALU.mult
+                out=offset[s][:], in0=mean_var[s][:, 0:1], scalar1=rstd[s][:], scalar2=-1.0, op0=ALU.mult, op1=ALU.mult
+            )
+            nc.gpsimd.tensor_scalar(
+                out=x_hat[s][:], in0=x_rows[s][:], scalar1=rstd[s][:], scalar2=offset[s][:], op0=ALU.mult, op1=ALU.add
             )
 
         def turn(s):

@@ -71,24 +71,27 @@ def tile_timesformerlayer_pb_kernel(tc, x_res, ln1_g, ln1_b, s_qkv_w, s_qkv_b, o
             load_rows(1)
             load_weights(0)
             load_rows(2)
+            load_rows(3)
             load_bias(0)
             load_weights(1)
-            load_rows(3)
+            load_rows(4)
             load_bias(1)
             load_weights(2)
-            load_rows(4)
+            load_rows(5)
             load_bias(2)
             load_weights(3)
-            load_rows(5)
+            load_rows(6)
             load_bias(3)
             load_weights(4)
-            load_rows(6)
+            load_rows(7)
             load_bias(4)
             load_weights(5)
-            load_rows(7)
+            load_rows(8)
             load_bias(5)
-            for s in range(8, SEQ):
-                load_rows(s)
+            load_rows(9)
+            load_rows(10)
+            load_rows(11)
+            load_rows(12)
 
         ident = const.tile([P, P], F32)
         make_identity(nc, ident[:])
@@ -131,11 +134,16 @@ def tile_timesformerlayer_pb_kernel(tc, x_res, ln1_g, ln1_b, s_qkv_w, s_qkv_b, o
 
         def normalise(s):
             x_hat[s] = work.tile([P, D], F32, name="x_hat")
-            nc.gpsimd.tensor_scalar(
+            if s < 4:
+                nc.vector.tensor_scalar(
+                    out=x_hat[s][:], in0=x_rows[s][:], scalar1=mean_var[s][:, 0:1], scalar2=rstd[s][:], op0=ALU.subtract, op1=ALU.mult
+                )
+                return
+            nc.vector.tensor_scalar(
                 out=offset[s][:], in0=mean_var[s][:, 0:1], scalar1=rstd[s][:], scalar2=-1.0, op0=ALU.mult, op1=ALU.mult
             )
-            nc.gpsimd.tensor_scalar(
-                out=x_hat[s][:], in0=x_rows[s][:], scalar1=rstd[s][:], scalar2=offset[s][:], op0=ALU.mult, op1=ALU.add
+            nc.scalar.activation(
+                out=x_hat[s][:], in_=x_rows[s][:], func=ACT.Identity, bias=offset[s][:], scale=rstd[s][:]
             )
 
         def turn(s):
@@ -174,7 +182,7 @@ def tile_timesformerlayer_pb_kernel(tc, x_res, ln1_g, ln1_b, s_qkv_w, s_qkv_b, o
 
         def group_weights(n, c):
             w_grouped[n, c] = work.tile([P, N_TILE, PACK], BF16, name="w_grouped%d" % c, align_bytes=64)
-            if c == 1:
+            if False:
                 nc.gpsimd.tensor_scalar(
                     out=w_grouped[n, c][:],
                     in0=w_raw[n][:, c * PACK : (c + 1) * PACK, :].rearrange("p t n -> p n t"),
@@ -183,7 +191,7 @@ def tile_timesformerlayer_pb_kernel(tc, x_res, ln1_g, ln1_b, s_qkv_w, s_qkv_b, o
                     op0=ALU.mult,
                     op1=ALU.add,
                 )
-            elif n < 3:
+            elif c==0:
                 nc.vector.tensor_copy(
                     out=w_grouped[n, c][:].rearrange("p (q i) t -> p q t i", i=4),
                     in_=w_raw[n][:, c * PACK : (c + 1) * PACK, :].rearrange("p t (q i) -> p q t i", i=4),
@@ -220,7 +228,7 @@ def tile_timesformerlayer_pb_kernel(tc, x_res, ln1_g, ln1_b, s_qkv_w, s_qkv_b, o
                 )
             part = result[:, place * N_TILE : (place + 1) * N_TILE]
             bias_part = bias_rows[:, n * N_TILE : (n + 1) * N_TILE]
-            if state["banks"] % SHARE != SHARE - 1:
+            if (state["banks"] % 6 != 5 or s < 0 or s == SEQ - 1):
                 nc.vector.tensor_tensor(out=part, in0=acc[:], in1=bias_part, op=ALU.add)
             else:
                 nc.scalar.copy(out=part, in_=acc[:])
@@ -232,43 +240,51 @@ def tile_timesformerlayer_pb_kernel(tc, x_res, ln1_g, ln1_b, s_qkv_w, s_qkv_b, o
                     out=out[:, s, first * N_TILE : (first + count) * N_TILE], in_=result[:, 0 : count * N_TILE]
                 )
 
+        due = [0, 1, 2, 3, 4, 5]
+
         def new_products(step):
             if step < 0:
                 return []
-            column = [(s, step, 1) for s in range(step)] if step < W_CHUNKS else []
-            chunks = min(step + 1, W_CHUNKS)
-            row = [(step, first, min(STORE_CHUNKS, chunks - first)) for first in range(0, chunks, STORE_CHUNKS)]
+            column = [(s, n, 0, 1) for n in range(W_CHUNKS) if due[n] == step for s in range(step)]
+            chunks = len([n for n in range(W_CHUNKS) if due[n] <= step])
+            run = 1 if step == SEQ - 1 else STORE_CHUNKS
+            row = [(step, n, n % run, min(run, chunks - n // run * run)) for n in range(chunks)]
             return column + row
 
         with tc.manual_schedule():
             for step in range(FIRST_STEP, SEQ):
-                banks = [(s, first + i, i, count) for s, first, count in new_products(step) for i in range(count)]
+                banks = new_products(step)
                 tasks = []
 
                 def add(ahead, limit, f, *args):
                     if 0 <= step + ahead < limit:
                         tasks.append(lambda: f(step + ahead, *args))
 
+                def addw(ahead, f, *args):
+                    for n in range(W_CHUNKS):
+                        if due[n] == step + ahead:
+                            tasks.append(lambda n=n: f(n, *args))
+
                 add(3, SEQ, row_scale)
                 add(3, SEQ, normalise)
                 add(1, SEQ, pack_rows)
-                add(2, W_CHUNKS, group_weights, 0)
-                add(2, W_CHUNKS, group_weights, 1)
-                add(1, W_CHUNKS, pack_weights, 0)
+                addw(1, pack_weights, 0)
+                addw(1, pack_weights, 1)
+                add(4, SEQ, row_sums, 0)
+                add(4, SEQ, row_sums, 1)
                 add(2, SEQ, turn)
                 add(2, SEQ, gain_and_shift, 0)
-                add(4, SEQ, row_sums, 0)
                 add(2, SEQ, gain_and_shift, 1)
+                addw(2, group_weights, 1)
                 add(2, SEQ, group_rows)
-                add(1, W_CHUNKS, pack_weights, 1)
-                add(4, SEQ, row_sums, 1)
+                addw(2, group_weights, 0)
                 add(4, SEQ, row_moments)
                 if step == FIRST_STEP + 1:
                     tasks.append(turn_gain_shift)
                 done = 0
                 for b, bank in enumerate(banks):
                     multiply(*bank)
-                    upto = ((b + 1) * len(tasks)) // len(banks)
+                    upto = -((-(b + 1) * len(tasks)) // len(banks))
                     for task in tasks[done:upto]:
                         task()
                     done = upto

@@ -22,7 +22,7 @@ K_CHUNKS = D // P
 N_TILE = 512
 W_CHUNKS = D3 // N_TILE
 EPS = 1e-6
-FIRST_STEP = -5
+FIRST_STEP = -8
 STORE_CHUNKS = 3
 FLOPS = 2 * P * SEQ * D * D3
 SHARE = 4
@@ -61,6 +61,11 @@ def tile_timesformerlayer_pb_kernel(tc, x_res, ln1_g, ln1_b, s_qkv_w, s_qkv_b, o
             cols = slice(n * N_TILE, (n + 1) * N_TILE)
             nc.sync.dma_start(out=w_raw[n][:], in_=w_view[:, :, cols])
 
+        def load_half(n, c):
+            cols = slice(n * N_TILE, (n + 1) * N_TILE)
+            rows = slice(c * PACK, (c + 1) * PACK)
+            nc.sync.dma_start(out=w_raw[n][:, rows, :], in_=w_view[:, rows, cols])
+
         def load_bias(n):
             cols = slice(n * N_TILE, (n + 1) * N_TILE)
             nc.sync.dma_start(out=bias_rows[:, cols], in_=s_qkv_b[cols].partition_broadcast(P))
@@ -71,27 +76,24 @@ def tile_timesformerlayer_pb_kernel(tc, x_res, ln1_g, ln1_b, s_qkv_w, s_qkv_b, o
             load_rows(1)
             load_weights(0)
             load_rows(2)
-            load_rows(3)
-            load_bias(0)
             load_weights(1)
+            load_bias(0)
+            load_rows(3)
             load_rows(4)
-            load_bias(1)
             load_weights(2)
+            load_bias(1)
             load_rows(5)
-            load_bias(2)
             load_weights(3)
+            load_bias(2)
             load_rows(6)
-            load_bias(3)
             load_weights(4)
+            load_bias(3)
             load_rows(7)
-            load_bias(4)
             load_weights(5)
-            load_rows(8)
+            load_bias(4)
             load_bias(5)
-            load_rows(9)
-            load_rows(10)
-            load_rows(11)
-            load_rows(12)
+            for s in range(8, SEQ):
+                load_rows(s)
 
         ident = const.tile([P, P], F32)
         make_identity(nc, ident[:])
@@ -132,16 +134,19 @@ def tile_timesformerlayer_pb_kernel(tc, x_res, ln1_g, ln1_b, s_qkv_w, s_qkv_b, o
                 out=rstd[s][:], in_=mean_var[s][:, 1:2], func=ACT.Abs_reciprocal_sqrt, bias=eps[:], scale=1.0
             )
 
+        def row_offset(s):
+            if not (s < 2):
+                nc.vector.tensor_scalar(
+                    out=offset[s][:], in0=mean_var[s][:, 0:1], scalar1=rstd[s][:], scalar2=-1.0, op0=ALU.mult, op1=ALU.mult
+                )
+
         def normalise(s):
             x_hat[s] = work.tile([P, D], F32, name="x_hat")
-            if s < 4:
+            if s < 2:
                 nc.vector.tensor_scalar(
                     out=x_hat[s][:], in0=x_rows[s][:], scalar1=mean_var[s][:, 0:1], scalar2=rstd[s][:], op0=ALU.subtract, op1=ALU.mult
                 )
                 return
-            nc.vector.tensor_scalar(
-                out=offset[s][:], in0=mean_var[s][:, 0:1], scalar1=rstd[s][:], scalar2=-1.0, op0=ALU.mult, op1=ALU.mult
-            )
             nc.scalar.activation(
                 out=x_hat[s][:], in_=x_rows[s][:], func=ACT.Identity, bias=offset[s][:], scale=rstd[s][:]
             )
@@ -165,10 +170,19 @@ def tile_timesformerlayer_pb_kernel(tc, x_res, ln1_g, ln1_b, s_qkv_w, s_qkv_b, o
                     scale=gain_shift[:, j : j + 1],
                 )
 
-        def group_rows(s):
+        def group_rows(s, engine):
+            chosen = "G" if False else "V" if False else "S"
+            if engine != chosen:
+                return
             y_grouped[s] = work.tile([P, PASSES, P, PACK], BF16, name="y_grouped", align_bytes=64)
+            if engine == "G":
+                nc.gpsimd.tensor_scalar(
+                    out=y_grouped[s][:], in0=y_turned[s][:].rearrange("p c t r -> p c r t"), scalar1=1.0, scalar2=0.0, op0=ALU.mult, op1=ALU.add
+                )
+                return
             for c in range(PASSES):
-                nc.scalar.copy(
+                copy = nc.vector.tensor_copy if engine == "V" else nc.scalar.copy
+                copy(
                     out=y_grouped[s][:, c, :, :].rearrange("p (q i) t -> p q t i", i=4),
                     in_=y_turned[s][:, c, :, :].rearrange("p t (q i) -> p q t i", i=4),
                 )
@@ -183,15 +197,17 @@ def tile_timesformerlayer_pb_kernel(tc, x_res, ln1_g, ln1_b, s_qkv_w, s_qkv_b, o
         def group_weights(n, c):
             w_grouped[n, c] = work.tile([P, N_TILE, PACK], BF16, name="w_grouped%d" % c, align_bytes=64)
             if False:
-                nc.gpsimd.tensor_scalar(
-                    out=w_grouped[n, c][:],
-                    in0=w_raw[n][:, c * PACK : (c + 1) * PACK, :].rearrange("p t n -> p n t"),
-                    scalar1=1.0,
-                    scalar2=0.0,
-                    op0=ALU.mult,
-                    op1=ALU.add,
-                )
-            elif c==0:
+                for part in range(4):
+                    cols = slice(part * N_TILE // 4, (part + 1) * N_TILE // 4)
+                    nc.gpsimd.tensor_scalar(
+                        out=w_grouped[n, c][:, cols, :],
+                        in0=w_raw[n][:, c * PACK : (c + 1) * PACK, cols].rearrange("p t n -> p n t"),
+                        scalar1=1.0,
+                        scalar2=0.0,
+                        op0=ALU.mult,
+                        op1=ALU.add,
+                    )
+            elif c == 0:
                 nc.vector.tensor_copy(
                     out=w_grouped[n, c][:].rearrange("p (q i) t -> p q t i", i=4),
                     in_=w_raw[n][:, c * PACK : (c + 1) * PACK, :].rearrange("p t (q i) -> p q t i", i=4),
@@ -228,7 +244,7 @@ def tile_timesformerlayer_pb_kernel(tc, x_res, ln1_g, ln1_b, s_qkv_w, s_qkv_b, o
                 )
             part = result[:, place * N_TILE : (place + 1) * N_TILE]
             bias_part = bias_rows[:, n * N_TILE : (n + 1) * N_TILE]
-            if (state["banks"] % 6 != 5 or s < 0 or s == SEQ - 1):
+            if not (max(s, n) >= 4 and ((s+n)%3==2 if s < 6 else (s+n)%6==5) and s < SEQ - 1):
                 nc.vector.tensor_tensor(out=part, in0=acc[:], in1=bias_part, op=ALU.add)
             else:
                 nc.scalar.copy(out=part, in_=acc[:])
@@ -265,26 +281,44 @@ def tile_timesformerlayer_pb_kernel(tc, x_res, ln1_g, ln1_b, s_qkv_w, s_qkv_b, o
                         if due[n] == step + ahead:
                             tasks.append(lambda n=n: f(n, *args))
 
-                add(3, SEQ, row_scale)
-                add(3, SEQ, normalise)
-                add(1, SEQ, pack_rows)
-                addw(1, pack_weights, 0)
-                addw(1, pack_weights, 1)
-                add(4, SEQ, row_sums, 0)
-                add(4, SEQ, row_sums, 1)
-                add(2, SEQ, turn)
-                add(2, SEQ, gain_and_shift, 0)
-                add(2, SEQ, gain_and_shift, 1)
-                addw(2, group_weights, 1)
-                add(2, SEQ, group_rows)
-                addw(2, group_weights, 0)
-                add(4, SEQ, row_moments)
-                if step == FIRST_STEP + 1:
+                if step < 0:
+                    add(3, SEQ, row_scale)
+                    add(3, SEQ, row_offset)
+                    add(2, SEQ, turn)
+                    add(2, SEQ, gain_and_shift, 0)
+                    add(2, SEQ, gain_and_shift, 1)
+                    add(3, SEQ, normalise)
+                    addw(2, group_weights, 1)
+                    add(2, SEQ, group_rows, "S")
+                    addw(2, group_weights, 0)
+                    addw(1, pack_weights, 0)
+                    addw(1, pack_weights, 1)
+                    add(1, SEQ, pack_rows)
+                    add(4, SEQ, row_sums, 0)
+                    add(4, SEQ, row_sums, 1)
+                    add(4, SEQ, row_moments)
+                else:
+                    add(3, SEQ, row_scale)
+                    addw(1, pack_weights, 0)
+                    add(4, SEQ, row_sums, 0)
+                    add(3, SEQ, row_offset)
+                    addw(1, pack_weights, 1)
+                    add(2, SEQ, turn)
+                    add(2, SEQ, gain_and_shift, 0)
+                    addw(2, group_weights, 1)
+                    add(1, SEQ, pack_rows)
+                    add(2, SEQ, gain_and_shift, 1)
+                    add(3, SEQ, normalise)
+                    add(2, SEQ, group_rows, "S")
+                    add(4, SEQ, row_sums, 1)
+                    addw(2, group_weights, 0)
+                    add(4, SEQ, row_moments)
+                if step == -4:
                     tasks.append(turn_gain_shift)
                 done = 0
                 for b, bank in enumerate(banks):
                     multiply(*bank)
-                    upto = -((-(b + 1) * len(tasks)) // len(banks))
+                    upto = min(len(tasks), -((-(b + 1) * len(tasks)) // max(1, int(len(banks) * 0.6))))
                     for task in tasks[done:upto]:
                         task()
                     done = upto

@@ -15,6 +15,7 @@ P = 128
 PACK = 4
 SAMPLES, FRAMES, PATCHES = 16, 8, 12
 SEQ = 1 + PATCHES
+CLS = 0
 D = 1024
 D3 = 3072
 PASSES = D // (P * PACK)
@@ -24,8 +25,13 @@ W_CHUNKS = D3 // N_TILE
 EPS = 1e-6
 FIRST_STEP = -8
 STORE_CHUNKS = 3
+CLS_COPIES = 2
+CLS_COLS = SAMPLES * CLS_COPIES
+CLS_PARTS = P // SAMPLES
+CLS_RUN = D3 // CLS_PARTS
+CLS_TURNS = CLS_RUN // P
+CLS_HALF = CLS_PARTS // 2
 FLOPS = 2 * P * SEQ * D * D3
-SHARE = 4
 
 
 def tile_timesformerlayer_pb_kernel(tc, x_res, ln1_g, ln1_b, s_qkv_w, s_qkv_b, out):
@@ -39,19 +45,22 @@ def tile_timesformerlayer_pb_kernel(tc, x_res, ln1_g, ln1_b, s_qkv_w, s_qkv_b, o
         acc_psum = ctx.enter_context(tc.psum_pool(name="acc_psum", bufs=6))
 
         w_view = s_qkv_w.rearrange("(j p) n -> p j n", p=P)
-        x_rows = [keep.tile([P, D], BF16, name="x%d" % s) for s in range(SEQ)]
+        x_rows = [keep.tile([P, D], BF16, name="x%d" % i) for i in range(SEQ)]
         w_raw = [keep.tile([P, K_CHUNKS, N_TILE], BF16, name="w_raw%d" % n) for n in range(W_CHUNKS)]
         bias_rows = const.tile([P, D3], BF16)
+        class_bias = const.tile([P, CLS_RUN], BF16)
         gs_rows_bf = const.tile([P, P], BF16)
         nc.vector.memset(gs_rows_bf[:], 0.0)
 
-        def load_rows(s):
-            if s == 0:
+        def patch(i):
+            return i if i < CLS else i - 1
+
+        def load_rows(i):
+            if i == CLS:
                 source = x_res[:, 0:1, :].to_broadcast([SAMPLES, FRAMES, D])
             else:
-                first = 1 + (s - 1) * FRAMES
-                source = x_res[:, first : first + FRAMES, :]
-            nc.sync.dma_start(out=x_rows[s][:], in_=source)
+                source = x_res[:, 1 + patch(i) * FRAMES : 1 + (patch(i) + 1) * FRAMES, :]
+            nc.sync.dma_start(out=x_rows[i][:], in_=source)
 
         def load_gain_shift():
             nc.sync.dma_start(out=gs_rows_bf[0:K_CHUNKS, :], in_=ln1_g.rearrange("(j p) -> j p", p=P))
@@ -61,14 +70,13 @@ def tile_timesformerlayer_pb_kernel(tc, x_res, ln1_g, ln1_b, s_qkv_w, s_qkv_b, o
             cols = slice(n * N_TILE, (n + 1) * N_TILE)
             nc.sync.dma_start(out=w_raw[n][:], in_=w_view[:, :, cols])
 
-        def load_half(n, c):
-            cols = slice(n * N_TILE, (n + 1) * N_TILE)
-            rows = slice(c * PACK, (c + 1) * PACK)
-            nc.sync.dma_start(out=w_raw[n][:, rows, :], in_=w_view[:, rows, cols])
-
         def load_bias(n):
             cols = slice(n * N_TILE, (n + 1) * N_TILE)
             nc.sync.dma_start(out=bias_rows[:, cols], in_=s_qkv_b[cols].partition_broadcast(P))
+
+        def load_class_bias():
+            source = s_qkv_b.rearrange("(k c) -> k c", k=CLS_PARTS).unsqueeze(0).to_broadcast([SAMPLES, CLS_PARTS, CLS_RUN])
+            nc.sync.dma_start(out=class_bias[:], in_=source)
 
         with tc.manual_schedule():
             load_rows(0)
@@ -92,8 +100,12 @@ def tile_timesformerlayer_pb_kernel(tc, x_res, ln1_g, ln1_b, s_qkv_w, s_qkv_b, o
             load_weights(5)
             load_bias(4)
             load_bias(5)
-            for s in range(8, SEQ):
-                load_rows(s)
+            load_class_bias()
+            load_rows(8)
+            load_rows(9)
+            load_rows(10)
+            load_rows(11)
+            load_rows(12)
 
         ident = const.tile([P, P], F32)
         make_identity(nc, ident[:])
@@ -110,113 +122,103 @@ def tile_timesformerlayer_pb_kernel(tc, x_res, ln1_g, ln1_b, s_qkv_w, s_qkv_b, o
 
         w_codes = keep.tile([P, W_CHUNKS, PASSES, N_TILE], U32, align_bytes=64)
         w_scales = keep.tile([P, W_CHUNKS, PASSES, N_TILE], U8, align_bytes=64)
-        y_codes = [keep.tile([P, PASSES * P], U32, name="y_codes%d" % s, align_bytes=64) for s in range(SEQ)]
-        y_scales = [keep.tile([P, PASSES * P], U8, name="y_scales%d" % s, align_bytes=64) for s in range(SEQ)]
-        stats = [keep.tile([P, 2, 6], F32, name="stats%d" % s) for s in range(SEQ)]
-        mean_var = [keep.tile([P, 2], F32, name="mean_var%d" % s) for s in range(SEQ)]
-        rstd = [keep.tile([P, 1], F32, name="rstd%d" % s) for s in range(SEQ)]
-        offset = [keep.tile([P, 1], F32, name="offset%d" % s) for s in range(SEQ)]
+        y_codes = [keep.tile([P, PASSES * P], U32, name="y_codes%d" % i, align_bytes=64) for i in range(SEQ)]
+        y_scales = [keep.tile([P, PASSES * P], U8, name="y_scales%d" % i, align_bytes=64) for i in range(SEQ)]
+        nc.gpsimd.memset(y_codes[CLS][:], 0)
+        nc.gpsimd.memset(y_scales[CLS][:], 0)
+        stats = [keep.tile([P, 2, 6], F32, name="stats%d" % i) for i in range(SEQ)]
+        mean_var = [keep.tile([P, 2], F32, name="mean_var%d" % i) for i in range(SEQ)]
+        rstd = [keep.tile([P, 1], F32, name="rstd%d" % i) for i in range(SEQ)]
+        offset = [keep.tile([P, 1], F32, name="offset%d" % i) for i in range(SEQ)]
+        class_t = keep.tile([P, CLS_TURNS, SAMPLES, CLS_PARTS], F32, name="class_t")
+        class_out = keep.tile([P, CLS_RUN], F32, name="class_out")
         x_hat = {}
         turned = {}
         y_turned = {}
         y_grouped = {}
         w_grouped = {}
 
-        def row_sums(s, h):
+        def row_sums(i, h):
             half = D // 2
-            nc.vector.bn_stats(out=stats[s][:, h, :], in_=x_rows[s][:, h * half : (h + 1) * half])
+            nc.vector.bn_stats(out=stats[i][:, h, :], in_=x_rows[i][:, h * half : (h + 1) * half])
 
-        def row_moments(s):
-            nc.vector.bn_aggr(out=mean_var[s][:], in_=stats[s][:].rearrange("p h c -> p (h c)"))
+        def row_moments(i):
+            nc.vector.bn_aggr(out=mean_var[i][:], in_=stats[i][:].rearrange("p h c -> p (h c)"))
 
-        def row_scale(s):
+        def row_scale(i):
             nc.scalar.activation(
-                out=rstd[s][:], in_=mean_var[s][:, 1:2], func=ACT.Abs_reciprocal_sqrt, bias=eps[:], scale=1.0
+                out=rstd[i][:], in_=mean_var[i][:, 1:2], func=ACT.Abs_reciprocal_sqrt, bias=eps[:], scale=1.0
             )
 
-        def row_offset(s):
-            if not (s < 2):
+        def row_offset(i):
+            if not (i < 4):
                 nc.vector.tensor_scalar(
-                    out=offset[s][:], in0=mean_var[s][:, 0:1], scalar1=rstd[s][:], scalar2=-1.0, op0=ALU.mult, op1=ALU.mult
+                    out=offset[i][:], in0=mean_var[i][:, 0:1], scalar1=rstd[i][:], scalar2=-1.0, op0=ALU.mult, op1=ALU.mult
                 )
 
-        def normalise(s):
-            x_hat[s] = work.tile([P, D], F32, name="x_hat")
-            if s < 2:
+        def normalise(i):
+            x_hat[i] = work.tile([P, D], F32, name="x_hat")
+            if i < 4:
                 nc.vector.tensor_scalar(
-                    out=x_hat[s][:], in0=x_rows[s][:], scalar1=mean_var[s][:, 0:1], scalar2=rstd[s][:], op0=ALU.subtract, op1=ALU.mult
+                    out=x_hat[i][:], in0=x_rows[i][:], scalar1=mean_var[i][:, 0:1], scalar2=rstd[i][:], op0=ALU.subtract, op1=ALU.mult
                 )
                 return
             nc.scalar.activation(
-                out=x_hat[s][:], in_=x_rows[s][:], func=ACT.Identity, bias=offset[s][:], scale=rstd[s][:]
+                out=x_hat[i][:], in_=x_rows[i][:], func=ACT.Identity, bias=offset[i][:], scale=rstd[i][:]
             )
 
-        def turn(s):
+        def turn(i):
             for c in range(PASSES):
-                turned[s, c] = turn_psum.tile([P, PACK, P], F32, name="turned", tag="turned")
+                turned[i, c] = turn_psum.tile([P, PACK, P], F32, name="turned", tag="turned")
                 for t in range(PACK):
                     j = c * PACK + t
-                    nc.tensor.transpose(turned[s, c][:, t, :], x_hat[s][:, j * P : (j + 1) * P], ident[:])
-            y_turned[s] = work.tile([P, PASSES, PACK, P], BF16, name="y_turned")
+                    nc.tensor.transpose(turned[i, c][:, t, :], x_hat[i][:, j * P : (j + 1) * P], ident[:])
+            cols = CLS_COLS if i == CLS else P
+            y_turned[i] = work.tile([P, PACK, PASSES, cols], BF16, name="y_turned%d" % cols)
 
-        def gain_and_shift(s, c):
+        def gain_and_shift(i, c):
+            step = FRAMES // CLS_COPIES if i == CLS else 1
             for t in range(PACK):
                 j = c * PACK + t
                 nc.scalar.activation(
-                    out=y_turned[s][:, c, t, :],
-                    in_=turned[s, c][:, t, :],
+                    out=y_turned[i][:, t, c, :],
+                    in_=turned[i, c][:, t, ::step],
                     func=ACT.Identity,
                     bias=gain_shift[:, K_CHUNKS + j : K_CHUNKS + j + 1],
                     scale=gain_shift[:, j : j + 1],
                 )
 
-        def group_rows(s, engine):
-            chosen = "G" if False else "V" if False else "S"
-            if engine != chosen:
-                return
-            y_grouped[s] = work.tile([P, PASSES, P, PACK], BF16, name="y_grouped", align_bytes=64)
-            if engine == "G":
-                nc.gpsimd.tensor_scalar(
-                    out=y_grouped[s][:], in0=y_turned[s][:].rearrange("p c t r -> p c r t"), scalar1=1.0, scalar2=0.0, op0=ALU.mult, op1=ALU.add
-                )
-                return
-            for c in range(PASSES):
-                copy = nc.vector.tensor_copy if engine == "V" else nc.scalar.copy
-                copy(
-                    out=y_grouped[s][:, c, :, :].rearrange("p (q i) t -> p q t i", i=4),
-                    in_=y_turned[s][:, c, :, :].rearrange("p t (q i) -> p q t i", i=4),
-                )
+        def group_rows(i):
+            cols = CLS_COLS if i == CLS else P
+            y_grouped[i] = work.tile([P, PASSES * cols, PACK], BF16, name="y_grouped%d" % cols, align_bytes=64)
+            nc.scalar.copy(
+                out=y_grouped[i][:].rearrange("p (q i) t -> p q t i", i=4),
+                in_=y_turned[i][:].rearrange("p t c r -> p t (c r)").rearrange("p t (q i) -> p q t i", i=4),
+            )
 
-        def pack_rows(s):
+        def pack_rows(i):
+            if i == CLS:
+                for c in range(PASSES):
+                    cols = slice(c * P, c * P + CLS_COLS)
+                    nc.vector.quantize_mx(
+                        out=y_codes[i][:, cols].bitcast(FP8X4),
+                        scales=y_scales[i][:, cols],
+                        in_=y_grouped[i][:, c * CLS_COLS : (c + 1) * CLS_COLS, :].rearrange("p r t -> p (r t)"),
+                    )
+                return
             nc.vector.quantize_mx(
-                out=y_codes[s][:].bitcast(FP8X4),
-                scales=y_scales[s][:],
-                in_=y_grouped[s][:].rearrange("p c r t -> p (c r t)"),
+                out=y_codes[i][:].bitcast(FP8X4),
+                scales=y_scales[i][:],
+                in_=y_grouped[i][:].rearrange("p r t -> p (r t)"),
             )
 
         def group_weights(n, c):
             w_grouped[n, c] = work.tile([P, N_TILE, PACK], BF16, name="w_grouped%d" % c, align_bytes=64)
-            if False:
-                for part in range(4):
-                    cols = slice(part * N_TILE // 4, (part + 1) * N_TILE // 4)
-                    nc.gpsimd.tensor_scalar(
-                        out=w_grouped[n, c][:, cols, :],
-                        in0=w_raw[n][:, c * PACK : (c + 1) * PACK, cols].rearrange("p t n -> p n t"),
-                        scalar1=1.0,
-                        scalar2=0.0,
-                        op0=ALU.mult,
-                        op1=ALU.add,
-                    )
-            elif c == 0:
-                nc.vector.tensor_copy(
-                    out=w_grouped[n, c][:].rearrange("p (q i) t -> p q t i", i=4),
-                    in_=w_raw[n][:, c * PACK : (c + 1) * PACK, :].rearrange("p t (q i) -> p q t i", i=4),
-                )
-            else:
-                nc.scalar.copy(
-                    out=w_grouped[n, c][:].rearrange("p (q i) t -> p q t i", i=4),
-                    in_=w_raw[n][:, c * PACK : (c + 1) * PACK, :].rearrange("p t (q i) -> p q t i", i=4),
-                )
+            copy = nc.vector.tensor_copy if c == 0 else nc.scalar.copy
+            copy(
+                out=w_grouped[n, c][:].rearrange("p (q i) t -> p q t i", i=4),
+                in_=w_raw[n][:, c * PACK : (c + 1) * PACK, :].rearrange("p t (q i) -> p q t i", i=4),
+            )
 
         def pack_weights(n, c):
             nc.vector.quantize_mx(
@@ -225,18 +227,18 @@ def tile_timesformerlayer_pb_kernel(tc, x_res, ln1_g, ln1_b, s_qkv_w, s_qkv_b, o
                 in_=w_grouped[n, c][:].rearrange("p n t -> p (n t)"),
             )
 
-        state = {"banks": 0, "result": None}
+        state = {"result": None}
 
-        def multiply(s, n, place, count):
+        def multiply(i, n, place, count):
             if place == 0:
-                state["result"] = (results.tile([P, count * N_TILE], F32, name="result%d" % count, bufs=[8,3,5][count - 1]))
+                state["result"] = results.tile([P, count * N_TILE], F32, name="result%d" % count, bufs=[8, 2, 5][count - 1])
             result = state["result"]
-            acc = acc_psum.tile([P, N_TILE], F32, name="acc")
+            acc = acc_psum.tile([P, N_TILE], F32, name="acc", tag="acc")
             for c in range(PASSES):
                 nc.tensor.matmul_mx(
                     out=acc[:],
-                    lhsT=y_codes[s][:, c * P : (c + 1) * P].bitcast(FP8X4),
-                    lhsT_scale=y_scales[s][:, c * P : (c + 1) * P],
+                    lhsT=y_codes[i][:, c * P : (c + 1) * P].bitcast(FP8X4),
+                    lhsT_scale=y_scales[i][:, c * P : (c + 1) * P],
                     rhs=w_codes[:, n, c, :].bitcast(FP8X4),
                     rhs_scale=w_scales[:, n, c, :],
                     start=(c == 0),
@@ -244,77 +246,112 @@ def tile_timesformerlayer_pb_kernel(tc, x_res, ln1_g, ln1_b, s_qkv_w, s_qkv_b, o
                 )
             part = result[:, place * N_TILE : (place + 1) * N_TILE]
             bias_part = bias_rows[:, n * N_TILE : (n + 1) * N_TILE]
-            if not (max(s, n) >= 4 and ((s+n)%3==2 if s < 6 else (s+n)%6==5) and s < SEQ - 1):
-                nc.vector.tensor_tensor(out=part, in0=acc[:], in1=bias_part, op=ALU.add)
-            else:
+            if max(i, n) >= 4 and ((i + n) % 3 == 2 if i < 6 else (i + n) % 6 == 5) and i < SEQ - 1:
                 nc.scalar.copy(out=part, in_=acc[:])
                 nc.gpsimd.tensor_tensor(out=part, in0=part, in1=bias_part, op=ALU.add)
-            state["banks"] += 1
+            else:
+                nc.vector.tensor_tensor(out=part, in0=acc[:], in1=bias_part, op=ALU.add)
             if place == count - 1:
                 first = n - place
                 nc.sync.dma_start(
-                    out=out[:, s, first * N_TILE : (first + count) * N_TILE], in_=result[:, 0 : count * N_TILE]
+                    out=out[:, 1 + patch(i), first * N_TILE : (first + count) * N_TILE], in_=result[:, 0 : count * N_TILE]
                 )
 
-        due = [0, 1, 2, 3, 4, 5]
+        def multiply_class(half, g):
+            acc = acc_psum.tile([P, CLS_HALF, P], F32, name="class_acc", tag="acc")
+            for q in range(CLS_HALF):
+                first = (half * CLS_HALF + q) * CLS_RUN + g * P
+                n, col = first // N_TILE, first % N_TILE
+                for c in range(PASSES):
+                    nc.tensor.matmul_mx(
+                        out=acc[:, q, :],
+                        lhsT=w_codes[:, n, c, col : col + P].bitcast(FP8X4),
+                        lhsT_scale=w_scales[:, n, c, col : col + P],
+                        rhs=y_codes[CLS][:, c * P : (c + 1) * P].bitcast(FP8X4),
+                        rhs_scale=y_scales[CLS][:, c * P : (c + 1) * P],
+                        start=(c == 0),
+                        stop=(c == PASSES - 1),
+                    )
+            nc.scalar.copy(
+                out=class_t[:, g, :, half * CLS_HALF : (half + 1) * CLS_HALF],
+                in_=acc[:, :, 0:CLS_COLS:CLS_COPIES].rearrange("p q b -> p b q"),
+            )
+
+        def finish_class():
+            rows = turn_psum.tile([P, CLS_TURNS, P], F32, name="class_rows", tag="turned")
+            for g in range(CLS_TURNS):
+                nc.tensor.transpose(rows[:, g, :], class_t[:, g, :, :].rearrange("p b k -> p (b k)"), ident[:])
+            nc.vector.tensor_tensor(out=class_out[:], in0=rows[:].rearrange("p g n -> p (g n)"), in1=class_bias[:], op=ALU.add)
+            frames = out.rearrange("(b t) s n -> t b s n", t=FRAMES)
+            for t in range(FRAMES):
+                nc.sync.dma_start(
+                    out=frames[t, :, 0, :].rearrange("b (k c) -> b k c", k=CLS_PARTS), in_=class_out[:]
+                )
 
         def new_products(step):
             if step < 0:
                 return []
-            column = [(s, n, 0, 1) for n in range(W_CHUNKS) if due[n] == step for s in range(step)]
-            chunks = len([n for n in range(W_CHUNKS) if due[n] <= step])
-            run = 1 if step == SEQ - 1 else STORE_CHUNKS
-            row = [(step, n, n % run, min(run, chunks - n // run * run)) for n in range(chunks)]
+            column = [(i, step, 0, 1) for i in range(step) if i != CLS] if step < W_CHUNKS else []
+            chunks = min(step + 1, W_CHUNKS)
+            run = 1 if step >= SEQ - 1 else STORE_CHUNKS
+            row = [] if step == CLS else [(step, n, n % run, min(run, chunks - n // run * run)) for n in range(chunks)]
             return column + row
+
+        class_tasks = {
+            3: [(multiply_class, 0, 0), (multiply_class, 0, 1), (multiply_class, 0, 2)],
+            5: [(multiply_class, 1, 0), (multiply_class, 1, 1), (multiply_class, 1, 2)],
+            6: [(finish_class,)],
+        }
 
         with tc.manual_schedule():
             for step in range(FIRST_STEP, SEQ):
                 banks = new_products(step)
                 tasks = []
 
-                def add(ahead, limit, f, *args):
-                    if 0 <= step + ahead < limit:
+                def add(ahead, f, *args):
+                    if 0 <= step + ahead < SEQ:
                         tasks.append(lambda: f(step + ahead, *args))
 
                 def addw(ahead, f, *args):
-                    for n in range(W_CHUNKS):
-                        if due[n] == step + ahead:
-                            tasks.append(lambda n=n: f(n, *args))
+                    if 0 <= step + ahead < W_CHUNKS:
+                        tasks.append(lambda: f(step + ahead, *args))
 
                 if step < 0:
-                    add(3, SEQ, row_scale)
-                    add(3, SEQ, row_offset)
-                    add(2, SEQ, turn)
-                    add(2, SEQ, gain_and_shift, 0)
-                    add(2, SEQ, gain_and_shift, 1)
-                    add(3, SEQ, normalise)
+                    add(3, row_scale)
+                    add(3, row_offset)
+                    add(2, turn)
+                    add(2, gain_and_shift, 0)
+                    add(2, gain_and_shift, 1)
+                    add(3, normalise)
                     addw(2, group_weights, 1)
-                    add(2, SEQ, group_rows, "S")
+                    add(2, group_rows)
                     addw(2, group_weights, 0)
                     addw(1, pack_weights, 0)
                     addw(1, pack_weights, 1)
-                    add(1, SEQ, pack_rows)
-                    add(4, SEQ, row_sums, 0)
-                    add(4, SEQ, row_sums, 1)
-                    add(4, SEQ, row_moments)
+                    add(1, pack_rows)
+                    add(4, row_sums, 0)
+                    add(4, row_sums, 1)
+                    add(4, row_moments)
                 else:
-                    add(3, SEQ, row_scale)
+                    add(3, row_scale)
                     addw(1, pack_weights, 0)
-                    add(4, SEQ, row_sums, 0)
-                    add(3, SEQ, row_offset)
+                    add(4, row_sums, 0)
+                    add(3, row_offset)
                     addw(1, pack_weights, 1)
-                    add(2, SEQ, turn)
-                    add(2, SEQ, gain_and_shift, 0)
+                    add(2, turn)
+                    add(2, gain_and_shift, 0)
                     addw(2, group_weights, 1)
-                    add(1, SEQ, pack_rows)
-                    add(2, SEQ, gain_and_shift, 1)
-                    add(3, SEQ, normalise)
-                    add(2, SEQ, group_rows, "S")
-                    add(4, SEQ, row_sums, 1)
+                    add(1, pack_rows)
+                    add(2, gain_and_shift, 1)
+                    add(3, normalise)
+                    add(2, group_rows)
+                    add(4, row_sums, 1)
                     addw(2, group_weights, 0)
-                    add(4, SEQ, row_moments)
+                    add(4, row_moments)
                 if step == -4:
                     tasks.append(turn_gain_shift)
+                for k, task in enumerate(class_tasks.get(step, [])):
+                    tasks.insert(4 * (k + 1), lambda task=task: task[0](*task[1:]))
                 done = 0
                 for b, bank in enumerate(banks):
                     multiply(*bank)

@@ -30,7 +30,7 @@ CLS_COLS = SAMPLES * CLS_COPIES
 CLS_PARTS = P // SAMPLES
 CLS_RUN = D3 // CLS_PARTS
 CLS_TURNS = CLS_RUN // P
-CLS_HALF = CLS_PARTS // 2
+CLS_BLOCKS = N_TILE // P
 FLOPS = 2 * P * SEQ * D * D3
 
 
@@ -130,7 +130,7 @@ def tile_timesformerlayer_pb_kernel(tc, x_res, ln1_g, ln1_b, s_qkv_w, s_qkv_b, o
         mean_var = [keep.tile([P, 2], F32, name="mean_var%d" % i) for i in range(SEQ)]
         rstd = [keep.tile([P, 1], F32, name="rstd%d" % i) for i in range(SEQ)]
         offset = [keep.tile([P, 1], F32, name="offset%d" % i) for i in range(SEQ)]
-        class_t = keep.tile([P, CLS_TURNS, SAMPLES, CLS_PARTS], F32, name="class_t")
+        class_t = keep.tile([P, SAMPLES, D3 // P], F32, name="class_t")
         class_out = keep.tile([P, CLS_RUN], F32, name="class_out")
         x_hat = {}
         turned = {}
@@ -257,30 +257,30 @@ def tile_timesformerlayer_pb_kernel(tc, x_res, ln1_g, ln1_b, s_qkv_w, s_qkv_b, o
                     out=out[:, 1 + patch(i), first * N_TILE : (first + count) * N_TILE], in_=result[:, 0 : count * N_TILE]
                 )
 
-        def multiply_class(half, g):
-            acc = acc_psum.tile([P, CLS_HALF, P], F32, name="class_acc", tag="acc")
-            for q in range(CLS_HALF):
-                first = (half * CLS_HALF + q) * CLS_RUN + g * P
-                n, col = first // N_TILE, first % N_TILE
+        def multiply_class(n):
+            acc = acc_psum.tile([P, CLS_BLOCKS, P], F32, name="class_acc", tag="acc")
+            for q in range(CLS_BLOCKS):
+                cols = slice(q * P, (q + 1) * P)
                 for c in range(PASSES):
                     nc.tensor.matmul_mx(
                         out=acc[:, q, :],
-                        lhsT=w_codes[:, n, c, col : col + P].bitcast(FP8X4),
-                        lhsT_scale=w_scales[:, n, c, col : col + P],
+                        lhsT=w_codes[:, n, c, cols].bitcast(FP8X4),
+                        lhsT_scale=w_scales[:, n, c, cols],
                         rhs=y_codes[CLS][:, c * P : (c + 1) * P].bitcast(FP8X4),
                         rhs_scale=y_scales[CLS][:, c * P : (c + 1) * P],
                         start=(c == 0),
                         stop=(c == PASSES - 1),
                     )
             nc.scalar.copy(
-                out=class_t[:, g, :, half * CLS_HALF : (half + 1) * CLS_HALF],
+                out=class_t[:, :, n * CLS_BLOCKS : (n + 1) * CLS_BLOCKS],
                 in_=acc[:, :, 0:CLS_COLS:CLS_COPIES].rearrange("p q b -> p b q"),
             )
 
         def finish_class():
             rows = turn_psum.tile([P, CLS_TURNS, P], F32, name="class_rows", tag="turned")
+            blocks = class_t[:].rearrange("p b n -> p (b n)")
             for g in range(CLS_TURNS):
-                nc.tensor.transpose(rows[:, g, :], class_t[:, g, :, :].rearrange("p b k -> p (b k)"), ident[:])
+                nc.tensor.transpose(rows[:, g, :], blocks[:, g::CLS_TURNS], ident[:])
             nc.vector.tensor_tensor(out=class_out[:], in0=rows[:].rearrange("p g n -> p (g n)"), in1=class_bias[:], op=ALU.add)
             frames = out.rearrange("(b t) s n -> t b s n", t=FRAMES)
             for t in range(FRAMES):
@@ -298,8 +298,12 @@ def tile_timesformerlayer_pb_kernel(tc, x_res, ln1_g, ln1_b, s_qkv_w, s_qkv_b, o
             return column + row
 
         class_tasks = {
-            3: [(multiply_class, 0, 0), (multiply_class, 0, 1), (multiply_class, 0, 2)],
-            5: [(multiply_class, 1, 0), (multiply_class, 1, 1), (multiply_class, 1, 2)],
+            0: [(multiply_class, 0)],
+            1: [(multiply_class, 1)],
+            2: [(multiply_class, 2)],
+            3: [(multiply_class, 3)],
+            4: [(multiply_class, 4)],
+            5: [(multiply_class, 5)],
             6: [(finish_class,)],
         }
 

@@ -277,7 +277,7 @@ def tile_timesformerlayer_pb_kernel(tc, x_res, ln1_g, ln1_b, s_qkv_w, s_qkv_b, o
             )
 
         def finish_class():
-            rows = turn_psum.tile([P, CLS_TURNS, P], F32, name="class_rows", tag="turned")
+            rows = acc_psum.tile([P, CLS_TURNS, P], F32, name="class_rows", tag="acc")
             blocks = class_t[:].rearrange("p b n -> p (b n)")
             for g in range(CLS_TURNS):
                 nc.tensor.transpose(rows[:, g, :], blocks[:, g::CLS_TURNS], ident[:])

@@ -150,15 +150,18 @@ def tile_timesformerlayer_pb_kernel(tc, x_res, ln1_g, ln1_b, s_qkv_w, s_qkv_b, o
                 out=rstd[i][:], in_=mean_var[i][:, 1:2], func=ACT.Abs_reciprocal_sqrt, bias=eps[:], scale=1.0
             )
 
+        def on_vector(i):
+            return not 7 <= i <= 9
+
         def row_offset(i):
-            if not (i < 4):
+            if not on_vector(i):
                 nc.vector.tensor_scalar(
                     out=offset[i][:], in0=mean_var[i][:, 0:1], scalar1=rstd[i][:], scalar2=-1.0, op0=ALU.mult, op1=ALU.mult
                 )
 
         def normalise(i):
             x_hat[i] = work.tile([P, D], F32, name="x_hat")
-            if i < 4:
+            if on_vector(i):
                 nc.vector.tensor_scalar(
                     out=x_hat[i][:], in0=x_rows[i][:], scalar1=mean_var[i][:, 0:1], scalar2=rstd[i][:], op0=ALU.subtract, op1=ALU.mult
                 )
@@ -214,7 +217,7 @@ def tile_timesformerlayer_pb_kernel(tc, x_res, ln1_g, ln1_b, s_qkv_w, s_qkv_b, o
 
         def group_weights(n, c):
             w_grouped[n, c] = work.tile([P, N_TILE, PACK], BF16, name="w_grouped%d" % c, align_bytes=64)
-            copy = nc.vector.tensor_copy if c == 0 else nc.scalar.copy
+            copy = nc.vector.tensor_copy if c == 0 and n < W_CHUNKS - 1 else nc.scalar.copy
             copy(
                 out=w_grouped[n, c][:].rearrange("p (q i) t -> p q t i", i=4),
                 in_=w_raw[n][:, c * PACK : (c + 1) * PACK, :].rearrange("p t (q i) -> p q t i", i=4),
@@ -246,7 +249,7 @@ def tile_timesformerlayer_pb_kernel(tc, x_res, ln1_g, ln1_b, s_qkv_w, s_qkv_b, o
                 )
             part = result[:, place * N_TILE : (place + 1) * N_TILE]
             bias_part = bias_rows[:, n * N_TILE : (n + 1) * N_TILE]
-            if max(i, n) >= 4 and ((i + n) % 3 == 2 if i < 6 else (i + n) % 6 == 5) and i < SEQ - 1:
+            if max(i, n) >= 3 and ((i + n) % 3 == 1 if i < 6 else n == W_CHUNKS - 2 and i < 9):
                 nc.scalar.copy(out=part, in_=acc[:])
                 nc.gpsimd.tensor_tensor(out=part, in0=part, in1=bias_part, op=ALU.add)
             else:
@@ -298,13 +301,10 @@ def tile_timesformerlayer_pb_kernel(tc, x_res, ln1_g, ln1_b, s_qkv_w, s_qkv_b, o
             return column + row
 
         class_tasks = {
-            0: [(multiply_class, 0)],
-            1: [(multiply_class, 1)],
-            2: [(multiply_class, 2)],
+            2: [(multiply_class, 0), (multiply_class, 1), (multiply_class, 2)],
             3: [(multiply_class, 3)],
             4: [(multiply_class, 4)],
-            5: [(multiply_class, 5)],
-            6: [(finish_class,)],
+            5: [(multiply_class, 5), (finish_class,)],
         }
 
         with tc.manual_schedule():
@@ -322,36 +322,36 @@ def tile_timesformerlayer_pb_kernel(tc, x_res, ln1_g, ln1_b, s_qkv_w, s_qkv_b, o
 
                 if step < 0:
                     add(3, row_scale)
-                    add(3, row_offset)
-                    add(2, turn)
-                    add(2, gain_and_shift, 0)
-                    add(2, gain_and_shift, 1)
-                    add(3, normalise)
-                    addw(2, group_weights, 1)
-                    add(2, group_rows)
-                    addw(2, group_weights, 0)
                     addw(1, pack_weights, 0)
-                    addw(1, pack_weights, 1)
+                    add(2, turn)
+                    add(3, row_offset)
+                    add(2, gain_and_shift, 0)
+                    add(3, normalise)
                     add(1, pack_rows)
                     add(4, row_sums, 0)
                     add(4, row_sums, 1)
+                    add(2, gain_and_shift, 1)
+                    addw(2, group_weights, 1)
+                    addw(1, pack_weights, 1)
+                    add(2, group_rows)
+                    addw(2, group_weights, 0)
                     add(4, row_moments)
                 else:
                     add(3, row_scale)
-                    addw(1, pack_weights, 0)
-                    add(4, row_sums, 0)
-                    add(3, row_offset)
                     addw(1, pack_weights, 1)
+                    addw(1, pack_weights, 0)
+                    add(3, row_offset)
+                    add(4, row_sums, 0)
                     add(2, turn)
-                    add(2, gain_and_shift, 0)
-                    addw(2, group_weights, 1)
                     add(1, pack_rows)
+                    add(4, row_sums, 1)
+                    add(2, gain_and_shift, 0)
                     add(2, gain_and_shift, 1)
                     add(3, normalise)
-                    add(2, group_rows)
-                    add(4, row_sums, 1)
-                    addw(2, group_weights, 0)
                     add(4, row_moments)
+                    addw(2, group_weights, 1)
+                    addw(2, group_weights, 0)
+                    add(2, group_rows)
                 if step == -4:
                     tasks.append(turn_gain_shift)
                 for k, task in enumerate(class_tasks.get(step, [])):
@@ -359,7 +359,7 @@ def tile_timesformerlayer_pb_kernel(tc, x_res, ln1_g, ln1_b, s_qkv_w, s_qkv_b, o
                 done = 0
                 for b, bank in enumerate(banks):
                     multiply(*bank)
-                    upto = min(len(tasks), -((-(b + 1) * len(tasks)) // max(1, int(len(banks) * 0.6))))
+                    upto = min(len(tasks), -((-(b + 1) * len(tasks)) // max(1, int(len(banks) * 0.7))))
                     for task in tasks[done:upto]:
                         task()
                     done = upto

@@ -51,6 +51,10 @@ def tile_timesformerlayer_pb_kernel(tc, x_res, ln1_g, ln1_b, s_qkv_w, s_qkv_b, o
         class_bias = const.tile([P, CLS_RUN], BF16)
         gs_rows_bf = const.tile([P, P], BF16)
         nc.vector.memset(gs_rows_bf[:], 0.0)
+        bias_pad = const.tile([P, D3], BF16)
+        nc.gpsimd.memset(bias_pad[:].bitcast(U32), 0)
+        ones = const.tile([P, P], BF16)
+        nc.vector.memset(ones[:], 1.0)
 
         def patch(i):
             return i if i < CLS else i - 1
@@ -70,9 +74,8 @@ def tile_timesformerlayer_pb_kernel(tc, x_res, ln1_g, ln1_b, s_qkv_w, s_qkv_b, o
             cols = slice(n * N_TILE, (n + 1) * N_TILE)
             nc.sync.dma_start(out=w_raw[n][:], in_=w_view[:, :, cols])
 
-        def load_bias(n):
-            cols = slice(n * N_TILE, (n + 1) * N_TILE)
-            nc.sync.dma_start(out=bias_rows[:, cols], in_=s_qkv_b[cols].partition_broadcast(P))
+        def load_bias():
+            nc.sync.dma_start(out=bias_pad[0:1, :], in_=s_qkv_b.unsqueeze(0))
 
         def load_class_bias():
             source = s_qkv_b.rearrange("(k c) -> k c", k=CLS_PARTS).unsqueeze(0).to_broadcast([SAMPLES, CLS_PARTS, CLS_RUN])
@@ -82,24 +85,19 @@ def tile_timesformerlayer_pb_kernel(tc, x_res, ln1_g, ln1_b, s_qkv_w, s_qkv_b, o
             load_rows(0)
             load_gain_shift()
             load_rows(1)
+            load_bias()
             load_weights(0)
             load_rows(2)
             load_weights(1)
-            load_bias(0)
             load_rows(3)
             load_rows(4)
             load_weights(2)
-            load_bias(1)
             load_rows(5)
             load_weights(3)
-            load_bias(2)
             load_rows(6)
             load_weights(4)
-            load_bias(3)
             load_rows(7)
             load_weights(5)
-            load_bias(4)
-            load_bias(5)
             load_class_bias()
             load_rows(8)
             load_rows(9)
@@ -137,6 +135,20 @@ def tile_timesformerlayer_pb_kernel(tc, x_res, ln1_g, ln1_b, s_qkv_w, s_qkv_b, o
         y_turned = {}
         y_grouped = {}
         w_grouped = {}
+
+        def spread_bias(h):
+            cols = slice(2 * h * N_TILE, 2 * (h + 1) * N_TILE)
+            bank = acc_psum.tile([P, 2 * N_TILE], BF16, name="bias_bank", tag="acc")
+            for q in range(2):
+                first = (2 * h + q) * N_TILE
+                nc.tensor.matmul(
+                    bank[:, q * N_TILE : (q + 1) * N_TILE],
+                    lhsT=ones[:],
+                    rhs=bias_pad[:, first : first + N_TILE],
+                    start=True,
+                    stop=True,
+                )
+            nc.vector.tensor_copy(out=bias_rows[:, cols], in_=bank[:])
 
         def row_sums(i, h):
             half = D // 2
@@ -216,7 +228,7 @@ def tile_timesformerlayer_pb_kernel(tc, x_res, ln1_g, ln1_b, s_qkv_w, s_qkv_b, o
             )
 
         def group_weights(n, c):
-            w_grouped[n, c] = work.tile([P, N_TILE, PACK], BF16, name="w_grouped%d" % c, align_bytes=64)
+            w_grouped[n, c] = work.tile([P, N_TILE, PACK], BF16, name="w_grouped%d" % c, bufs=2, align_bytes=64)
             copy = nc.vector.tensor_copy if c == 0 and n < W_CHUNKS - 1 else nc.scalar.copy
             copy(
                 out=w_grouped[n, c][:].rearrange("p (q i) t -> p q t i", i=4),
@@ -354,6 +366,8 @@ def tile_timesformerlayer_pb_kernel(tc, x_res, ln1_g, ln1_b, s_qkv_w, s_qkv_b, o
                     add(2, group_rows)
                 if step == -4:
                     tasks.append(turn_gain_shift)
+                if step % 2 == 1 and -3 <= step <= 1:
+                    tasks.append(lambda: spread_bias((step + 3) // 2))
                 for k, task in enumerate(class_tasks.get(step, [])):
                     tasks.insert(4 * (k + 1), lambda task=task: task[0](*task[1:]))
                 done = 0

from contextlib import ExitStack

import concourse.mybir as mybir
from concourse.masks import make_identity

F32 = mybir.dt.float32
BF16 = mybir.dt.bfloat16
U32 = mybir.dt.uint32
U8 = mybir.dt.uint8
FP8X4 = mybir.dt.float8_e4m3fn_x4
ACT = mybir.ActivationFunctionType
ALU = mybir.AluOpType

P = 128
PACK = 4
SAMPLES, FRAMES, PATCHES = 16, 8, 12
SEQ = 1 + PATCHES
CLS = 0
D = 1024
D3 = 3072
PASSES = D // (P * PACK)
K_CHUNKS = D // P
N_TILE = 512
W_CHUNKS = D3 // N_TILE
EPS = 1e-6
FIRST_STEP = -8
STORE_CHUNKS = 3
CLS_COPIES = 2
CLS_COLS = SAMPLES * CLS_COPIES
CLS_PARTS = P // SAMPLES
CLS_RUN = D3 // CLS_PARTS
CLS_TURNS = CLS_RUN // P
CLS_BLOCKS = N_TILE // P
FLOPS = 2 * P * SEQ * D * D3


def tile_timesformerlayer_pb_kernel(tc, x_res, ln1_g, ln1_b, s_qkv_w, s_qkv_b, out):
    nc = tc.nc
    with ExitStack() as ctx:
        const = ctx.enter_context(tc.tile_pool(name="const", bufs=1))
        keep = ctx.enter_context(tc.tile_pool(name="keep", bufs=1))
        work = ctx.enter_context(tc.tile_pool(name="work", bufs=3))
        results = ctx.enter_context(tc.tile_pool(name="results", bufs=6))
        turn_psum = ctx.enter_context(tc.psum_pool(name="turn_psum", bufs=2))
        acc_psum = ctx.enter_context(tc.psum_pool(name="acc_psum", bufs=6))

        w_view = s_qkv_w.rearrange("(j p) n -> p j n", p=P)
        x_rows = [keep.tile([P, D], BF16, name="x%d" % i) for i in range(SEQ)]
        w_raw = [keep.tile([P, K_CHUNKS, N_TILE], BF16, name="w_raw%d" % n) for n in range(W_CHUNKS)]
        bias_rows = const.tile([P, D3], BF16)
        class_bias = const.tile([P, CLS_RUN], BF16)
        gs_rows_bf = const.tile([P, P], BF16)
        nc.vector.memset(gs_rows_bf[:], 0.0)
        bias_pad = const.tile([P, D3], BF16)
        nc.gpsimd.memset(bias_pad[:].bitcast(U32), 0)
        ones = const.tile([P, P], BF16)
        nc.vector.memset(ones[:], 1.0)

        def patch(i):
            return i if i < CLS else i - 1

        def load_rows(i):
            if i == CLS:
                source = x_res[:, 0:1, :].to_broadcast([SAMPLES, FRAMES, D])
            else:
                source = x_res[:, 1 + patch(i) * FRAMES : 1 + (patch(i) + 1) * FRAMES, :]
            nc.sync.dma_start(out=x_rows[i][:], in_=source)

        def load_gain_shift():
            nc.sync.dma_start(out=gs_rows_bf[0:K_CHUNKS, :], in_=ln1_g.rearrange("(j p) -> j p", p=P))
            nc.sync.dma_start(out=gs_rows_bf[K_CHUNKS : 2 * K_CHUNKS, :], in_=ln1_b.rearrange("(j p) -> j p", p=P))

        def load_weights(n):
            cols = slice(n * N_TILE, (n + 1) * N_TILE)
            nc.sync.dma_start(out=w_raw[n][:], in_=w_view[:, :, cols])

        def load_bias():
            nc.sync.dma_start(out=bias_pad[0:1, :], in_=s_qkv_b.unsqueeze(0))

        def load_class_bias():
            source = s_qkv_b.rearrange("(k c) -> k c", k=CLS_PARTS).unsqueeze(0).to_broadcast([SAMPLES, CLS_PARTS, CLS_RUN])
            nc.sync.dma_start(out=class_bias[:], in_=source)

        with tc.manual_schedule():
            load_rows(0)
            load_gain_shift()
            load_rows(1)
            load_bias()
            load_weights(0)
            load_rows(2)
            load_weights(1)
            load_rows(3)
            load_rows(4)
            load_weights(2)
            load_rows(5)
            load_weights(3)
            load_rows(6)
            load_weights(4)
            load_rows(7)
            load_weights(5)
            load_class_bias()
            load_rows(8)
            load_rows(9)
            load_rows(10)
            load_rows(11)
            load_rows(12)

        ident = const.tile([P, P], F32)
        make_identity(nc, ident[:])
        eps = const.tile([P, 1], F32)
        nc.vector.memset(eps[:], EPS)
        gs_rows = const.tile([P, P], F32)
        gain_shift = const.tile([P, 2 * K_CHUNKS], F32)

        def turn_gain_shift():
            nc.vector.tensor_copy(out=gs_rows[:], in_=gs_rows_bf[:])
            gs_turned = turn_psum.tile([P, PACK, P], F32, name="gs_turned", tag="turned")
            nc.tensor.transpose(gs_turned[:, 0, :], gs_rows[:], ident[:])
            nc.vector.tensor_copy(out=gain_shift[:], in_=gs_turned[:, 0, 0 : 2 * K_CHUNKS])

        w_codes = keep.tile([P, W_CHUNKS, PASSES, N_TILE], U32, align_bytes=64)
        w_scales = keep.tile([P, W_CHUNKS, PASSES, N_TILE], U8, align_bytes=64)
        y_codes = [keep.tile([P, PASSES * P], U32, name="y_codes%d" % i, align_bytes=64) for i in range(SEQ)]
        y_scales = [keep.tile([P, PASSES * P], U8, name="y_scales%d" % i, align_bytes=64) for i in range(SEQ)]
        nc.gpsimd.memset(y_codes[CLS][:], 0)
        nc.gpsimd.memset(y_scales[CLS][:], 0)
        stats = [keep.tile([P, 2, 6], F32, name="stats%d" % i) for i in range(SEQ)]
        mean_var = [keep.tile([P, 2], F32, name="mean_var%d" % i) for i in range(SEQ)]
        rstd = [keep.tile([P, 1], F32, name="rstd%d" % i) for i in range(SEQ)]
        offset = [keep.tile([P, 1], F32, name="offset%d" % i) for i in range(SEQ)]
        class_t = keep.tile([P, SAMPLES, D3 // P], F32, name="class_t")
        class_out = keep.tile([P, CLS_RUN], F32, name="class_out")
        x_hat = {}
        turned = {}
        y_turned = {}
        y_grouped = {}
        w_grouped = {}

        def spread_bias(h):
            cols = slice(2 * h * N_TILE, 2 * (h + 1) * N_TILE)
            bank = acc_psum.tile([P, 2 * N_TILE], BF16, name="bias_bank", tag="acc")
            for q in range(2):
                first = (2 * h + q) * N_TILE
                nc.tensor.matmul(
                    bank[:, q * N_TILE : (q + 1) * N_TILE],
                    lhsT=ones[:],
                    rhs=bias_pad[:, first : first + N_TILE],
                    start=True,
                    stop=True,
                )
            nc.vector.tensor_copy(out=bias_rows[:, cols], in_=bank[:])

        def row_sums(i, h):
            half = D // 2
            nc.vector.bn_stats(out=stats[i][:, h, :], in_=x_rows[i][:, h * half : (h + 1) * half])

        def row_moments(i):
            nc.vector.bn_aggr(out=mean_var[i][:], in_=stats[i][:].rearrange("p h c -> p (h c)"))

        def row_scale(i):
            nc.scalar.activation(
                out=rstd[i][:], in_=mean_var[i][:, 1:2], func=ACT.Abs_reciprocal_sqrt, bias=eps[:], scale=1.0
            )

        def on_vector(i):
            return not 7 <= i <= 9

        def row_offset(i):
            if not on_vector(i):
                nc.vector.tensor_scalar(
                    out=offset[i][:], in0=mean_var[i][:, 0:1], scalar1=rstd[i][:], scalar2=-1.0, op0=ALU.mult, op1=ALU.mult
                )

        def normalise(i):
            x_hat[i] = work.tile([P, D], F32, name="x_hat")
            if on_vector(i):
                nc.vector.tensor_scalar(
                    out=x_hat[i][:], in0=x_rows[i][:], scalar1=mean_var[i][:, 0:1], scalar2=rstd[i][:], op0=ALU.subtract, op1=ALU.mult
                )
                return
            nc.scalar.activation(
                out=x_hat[i][:], in_=x_rows[i][:], func=ACT.Identity, bias=offset[i][:], scale=rstd[i][:]
            )

        def turn(i):
            for c in range(PASSES):
                turned[i, c] = turn_psum.tile([P, PACK, P], F32, name="turned", tag="turned")
                for t in range(PACK):
                    j = c * PACK + t
                    nc.tensor.transpose(turned[i, c][:, t, :], x_hat[i][:, j * P : (j + 1) * P], ident[:])
            cols = CLS_COLS if i == CLS else P
            y_turned[i] = work.tile([P, PACK, PASSES, cols], BF16, name="y_turned%d" % cols)

        def gain_and_shift(i, c):
            step = FRAMES // CLS_COPIES if i == CLS else 1
            for t in range(PACK):
                j = c * PACK + t
                nc.scalar.activation(
                    out=y_turned[i][:, t, c, :],
                    in_=turned[i, c][:, t, ::step],
                    func=ACT.Identity,
                    bias=gain_shift[:, K_CHUNKS + j : K_CHUNKS + j + 1],
                    scale=gain_shift[:, j : j + 1],
                )

        def group_rows(i):
            cols = CLS_COLS if i == CLS else P
            y_grouped[i] = work.tile([P, PASSES * cols, PACK], BF16, name="y_grouped%d" % cols, align_bytes=64)
            nc.scalar.copy(
                out=y_grouped[i][:].rearrange("p (q i) t -> p q t i", i=4),
                in_=y_turned[i][:].rearrange("p t c r -> p t (c r)").rearrange("p t (q i) -> p q t i", i=4),
            )

        def pack_rows(i):
            if i == CLS:
                for c in range(PASSES):
                    cols = slice(c * P, c * P + CLS_COLS)
                    nc.vector.quantize_mx(
                        out=y_codes[i][:, cols].bitcast(FP8X4),
                        scales=y_scales[i][:, cols],
                        in_=y_grouped[i][:, c * CLS_COLS : (c + 1) * CLS_COLS, :].rearrange("p r t -> p (r t)"),
                    )
                return
            nc.vector.quantize_mx(
                out=y_codes[i][:].bitcast(FP8X4),
                scales=y_scales[i][:],
                in_=y_grouped[i][:].rearrange("p r t -> p (r t)"),
            )

        def group_weights(n, c):
            w_grouped[n, c] = work.tile([P, N_TILE, PACK], BF16, name="w_grouped%d" % c, bufs=2, align_bytes=64)
            copy = nc.vector.tensor_copy if c == 0 and n < W_CHUNKS - 1 else nc.scalar.copy
            copy(
                out=w_grouped[n, c][:].rearrange("p (q i) t -> p q t i", i=4),
                in_=w_raw[n][:, c * PACK : (c + 1) * PACK, :].rearrange("p t (q i) -> p q t i", i=4),
            )

        def pack_weights(n, c):
            nc.vector.quantize_mx(
                out=w_codes[:, n, c, :].bitcast(FP8X4),
                scales=w_scales[:, n, c, :],
                in_=w_grouped[n, c][:].rearrange("p n t -> p (n t)"),
            )

        state = {"result": None}

        def multiply(i, n, place, count):
            if place == 0:
                state["result"] = results.tile([P, count * N_TILE], F32, name="result%d" % count, bufs=[8, 2, 5][count - 1])
            result = state["result"]
            acc = acc_psum.tile([P, N_TILE], F32, name="acc", tag="acc")
            for c in range(PASSES):
                nc.tensor.matmul_mx(
                    out=acc[:],
                    lhsT=y_codes[i][:, c * P : (c + 1) * P].bitcast(FP8X4),
                    lhsT_scale=y_scales[i][:, c * P : (c + 1) * P],
                    rhs=w_codes[:, n, c, :].bitcast(FP8X4),
                    rhs_scale=w_scales[:, n, c, :],
                    start=(c == 0),
                    stop=(c == PASSES - 1),
                )
            part = result[:, place * N_TILE : (place + 1) * N_TILE]
            bias_part = bias_rows[:, n * N_TILE : (n + 1) * N_TILE]
            if max(i, n) >= 3 and ((i + n) % 3 == 1 if i < 6 else n == W_CHUNKS - 2 and i < 9):
                nc.scalar.copy(out=part, in_=acc[:])
                nc.gpsimd.tensor_tensor(out=part, in0=part, in1=bias_part, op=ALU.add)
            else:
                nc.vector.tensor_tensor(out=part, in0=acc[:], in1=bias_part, op=ALU.add)
            if place == count - 1:
                first = n - place
                nc.sync.dma_start(
                    out=out[:, 1 + patch(i), first * N_TILE : (first + count) * N_TILE], in_=result[:, 0 : count * N_TILE]
                )

        def multiply_class(n):
            acc = acc_psum.tile([P, CLS_BLOCKS, P], F32, name="class_acc", tag="acc")
            for q in range(CLS_BLOCKS):
                cols = slice(q * P, (q + 1) * P)
                for c in range(PASSES):
                    nc.tensor.matmul_mx(
                        out=acc[:, q, :],
                        lhsT=w_codes[:, n, c, cols].bitcast(FP8X4),
                        lhsT_scale=w_scales[:, n, c, cols],
                        rhs=y_codes[CLS][:, c * P : (c + 1) * P].bitcast(FP8X4),
                        rhs_scale=y_scales[CLS][:, c * P : (c + 1) * P],
                        start=(c == 0),
                        stop=(c == PASSES - 1),
                    )
            nc.scalar.copy(
                out=class_t[:, :, n * CLS_BLOCKS : (n + 1) * CLS_BLOCKS],
                in_=acc[:, :, 0:CLS_COLS:CLS_COPIES].rearrange("p q b -> p b q"),
            )

        def finish_class():
            rows = acc_psum.tile([P, CLS_TURNS, P], F32, name="class_rows", tag="acc")
            blocks = class_t[:].rearrange("p b n -> p (b n)")
            for g in range(CLS_TURNS):
                nc.tensor.transpose(rows[:, g, :], blocks[:, g::CLS_TURNS], ident[:])
            nc.vector.tensor_tensor(out=class_out[:], in0=rows[:].rearrange("p g n -> p (g n)"), in1=class_bias[:], op=ALU.add)
            frames = out.rearrange("(b t) s n -> t b s n", t=FRAMES)
            for t in range(FRAMES):
                nc.sync.dma_start(
                    out=frames[t, :, 0, :].rearrange("b (k c) -> b k c", k=CLS_PARTS), in_=class_out[:]
                )

        def new_products(step):
            if step < 0:
                return []
            column = [(i, step, 0, 1) for i in range(step) if i != CLS] if step < W_CHUNKS else []
            chunks = min(step + 1, W_CHUNKS)
            run = 1 if step >= SEQ - 1 else STORE_CHUNKS
            row = [] if step == CLS else [(step, n, n % run, min(run, chunks - n // run * run)) for n in range(chunks)]
            return column + row

        class_tasks = {
            2: [(multiply_class, 0), (multiply_class, 1), (multiply_class, 2)],
            3: [(multiply_class, 3)],
            4: [(multiply_class, 4)],
            5: [(multiply_class, 5), (finish_class,)],
        }

        with tc.manual_schedule():
            for step in range(FIRST_STEP, SEQ):
                banks = new_products(step)
                tasks = []

                def add(ahead, f, *args):
                    if 0 <= step + ahead < SEQ:
                        tasks.append(lambda: f(step + ahead, *args))

                def addw(ahead, f, *args):
                    if 0 <= step + ahead < W_CHUNKS:
                        tasks.append(lambda: f(step + ahead, *args))

                if step < 0:
                    add(3, row_scale)
                    addw(1, pack_weights, 0)
                    add(2, turn)
                    add(3, row_offset)
                    add(2, gain_and_shift, 0)
                    add(3, normalise)
                    add(1, pack_rows)
                    add(4, row_sums, 0)
                    add(4, row_sums, 1)
                    add(2, gain_and_shift, 1)
                    addw(2, group_weights, 1)
                    addw(1, pack_weights, 1)
                    add(2, group_rows)
                    addw(2, group_weights, 0)
                    add(4, row_moments)
                else:
                    add(3, row_scale)
                    addw(1, pack_weights, 1)
                    addw(1, pack_weights, 0)
                    add(3, row_offset)
                    add(4, row_sums, 0)
                    add(2, turn)
                    add(1, pack_rows)
                    add(4, row_sums, 1)
                    add(2, gain_and_shift, 0)
                    add(2, gain_and_shift, 1)
                    add(3, normalise)
                    add(4, row_moments)
                    addw(2, group_weights, 1)
                    addw(2, group_weights, 0)
                    add(2, group_rows)
                if step == -4:
                    tasks.append(turn_gain_shift)
                if step % 2 == 1 and -3 <= step <= 1:
                    tasks.append(lambda: spread_bias((step + 3) // 2))
                for k, task in enumerate(class_tasks.get(step, [])):
                    tasks.insert(4 * (k + 1), lambda task=task: task[0](*task[1:]))
                done = 0
                for b, bank in enumerate(banks):
                    multiply(*bank)
                    upto = min(len(tasks), -((-(b + 1) * len(tasks)) // max(1, int(len(banks) * 0.7))))
                    for task in tasks[done:upto]:
                        task()
                    done = upto
                for task in tasks[done:]:
                    task()
